import numpy as np
import ml_dtypes


def mxq(x, axis, fmt="e4m3"):
    dtype, down = {"e4m3": (ml_dtypes.float8_e4m3fn, 7), "e5m2": (ml_dtypes.float8_e5m2, 14)}[fmt]
    v = np.moveaxis(np.asarray(x, np.float32).astype(ml_dtypes.bfloat16).astype(np.float64), axis, -1)
    blocks = v.reshape(v.shape[:-1] + (-1, 32))
    amax = np.abs(blocks).max(-1, keepdims=True)
    byte = np.maximum(np.where(amax > 0, np.frexp(amax)[1] - 1 + 127, 0) - down, 1)
    scale = np.exp2(byte - 127.0)
    codes = (blocks / scale).astype(np.float32).astype(dtype).astype(np.float64)
    return np.moveaxis((codes * scale).reshape(v.shape), -1, axis)


WIDE = False


def mx_kscale(k):
    if not WIDE:
        return np.ones(k)
    levels = np.array([10, -10, 5, -5, 0])
    if k % 512:
        return np.exp2(np.random.permutation(np.resize(levels, k // 32))).repeat(32)
    a = np.empty((k // 512, 16))
    for p in range(k // 512):
        a[p, :8] = np.random.permutation(np.resize(levels, 8))
        for g in range(8):
            far = levels[np.abs(levels - a[p, g]) >= 10]
            a[p, g + 8] = far[np.random.randint(len(far))]
    return np.exp2(a.ravel()).repeat(32)


BF16 = ml_dtypes.bfloat16


def bf(x):
    return np.asarray(x, np.float32).astype(BF16)


def f64(x):
    return np.asarray(x).astype(np.float64)


B, S, H, NH = 4, 256, 1024, 16
LN_EPS = 1e-5


def silu(v):
    return v / (1.0 + np.exp(-v))


def setup_inputs():
    s, t = mx_kscale(H), mx_kscale(H)
    w = 1.0 / np.sqrt(H)
    z = (np.random.standard_normal((B, S, H)) + 0.3 * np.random.standard_normal((B, S, 1))) * 2.0 / S
    return {"z": bf(z),
            "hidden_states": bf(np.random.standard_normal((B, S, H)) * s),
            "Wg": bf(np.random.standard_normal((H, H)) * w / s[:, None]),
            "Wo": bf(np.random.standard_normal((H, H)) * w / t[:, None]),
            "gamma": bf((1.0 + 0.1 * np.random.standard_normal(H)) * t),
            "beta": bf(0.1 * np.random.standard_normal(H) * t)}


def reference(z, hidden_states, Wg, Wo, gamma, beta):
    z = f64(z)
    g = mxq(f64(hidden_states), 2, "e4m3") @ mxq(f64(Wg), 0, "e4m3")
    mu = np.mean(z, axis=-1, keepdims=True)
    var = np.mean(np.square(z - mu), axis=-1, keepdims=True)
    zn = (z - mu) * (1.0 / np.sqrt(var + LN_EPS)) * f64(gamma) + f64(beta)
    h = zn * silu(g)
    return mxq(h, 2, "e4m3") @ mxq(f64(Wo), 0, "e4m3")

@@ -1,0 +1,298 @@
+from contextlib import ExitStack
+
+import concourse.mybir as mybir
+from concourse.masks import make_identity
+
+F32 = mybir.dt.float32
+BF16 = mybir.dt.bfloat16
+U32 = mybir.dt.uint32
+U8 = mybir.dt.uint8
+FP8X4 = mybir.dt.float8_e4m3fn_x4
+ALU = mybir.AluOpType
+ACT = mybir.ActivationFunctionType
+
+P = 128
+PACK = 4
+K_PASS = P * PACK
+TOKENS = 1024
+H = 1024
+PASSES = H // K_PASS
+TOKEN_TILES = TOKENS // P
+FEATURE_TILES = H // P
+CHUNK_TILES = 2
+CHUNK = CHUNK_TILES * P
+CHUNKS = TOKENS // CHUNK
+N_OUT = 512
+LN_EPS = 1e-5
+W_PIECE = 512
+BN_WIDTH = 512
+
+FLOPS = 2 * 2 * TOKENS * H * H
+
+
+def tile_gatedlinearattention_pb_kernel(tc, z, hidden_states, Wg, Wo, gamma, beta, out):
+    nc = tc.nc
+    x_dram = hidden_states.flatten_outer_dims()
+    z_dram = z.flatten_outer_dims()
+    out_dram = out.flatten_outer_dims()
+
+    with ExitStack() as ctx:
+        ctx.enter_context(tc.manual_schedule())
+        keep = ctx.enter_context(tc.tile_pool(name="keep", bufs=1))
+        stage = ctx.enter_context(tc.tile_pool(name="stage", bufs=3))
+        small = ctx.enter_context(tc.tile_pool(name="small", bufs=TOKEN_TILES))
+        normed = ctx.enter_context(tc.tile_pool(name="normed", bufs=2 * CHUNK_TILES))
+        units = ctx.enter_context(tc.tile_pool(name="units", bufs=CHUNKS * PASSES))
+        result = ctx.enter_context(tc.tile_pool(name="result", bufs=6))
+        psum = ctx.enter_context(tc.psum_pool(name="psum", bufs=8))
+
+        def chunk_tiles(ch):
+            return range(ch * CHUNK_TILES, (ch + 1) * CHUNK_TILES)
+
+        z_all = keep.tile([P, TOKEN_TILES, H], BF16)
+        x_all = keep.tile([P, TOKEN_TILES * H], BF16)
+        wg_raw = keep.tile([P, PASSES, PACK, H], BF16)
+        wo_raw = keep.tile([P, PASSES, PACK, H], BF16)
+
+        def load_z(ch):
+            first = ch * CHUNK_TILES
+            nc.sync.dma_start(
+                out=z_all[:, first : first + CHUNK_TILES, :],
+                in_=z_dram[ch * CHUNK : (ch + 1) * CHUNK, :].rearrange("(t p) k -> p t k", p=P),
+            )
+
+        def load_x(ch):
+            nc.sync.dma_start(
+                out=x_all[:, ch * CHUNK_TILES * H : (ch + 1) * CHUNK_TILES * H].rearrange("p (t k) -> p t k", k=H),
+                in_=x_dram[ch * CHUNK : (ch + 1) * CHUNK, :].rearrange("(t p) k -> p t k", p=P),
+            )
+
+        gamma_raw = keep.tile([P, PASSES, PACK], BF16)
+        beta_raw = keep.tile([P, PASSES, PACK], BF16)
+
+        load_z(0)
+        load_x(0)
+        nc.sync.dma_start(out=gamma_raw[:], in_=gamma.rearrange("(c p t) -> p c t", p=P, t=PACK))
+        nc.sync.dma_start(out=beta_raw[:], in_=beta.rearrange("(c p t) -> p c t", p=P, t=PACK))
+        for ch in range(1, CHUNKS):
+            load_z(ch)
+            load_x(ch)
+        for raw, w_dram in ((wg_raw, Wg), (wo_raw, Wo)):
+            for c in range(PASSES):
+                nc.sync.dma_start(
+                    out=raw[:, c],
+                    in_=w_dram[c * K_PASS : (c + 1) * K_PASS, :].rearrange("(p j) n -> p j n", j=PACK),
+                )
+
+        neg_half = keep.tile([P, 1], F32)
+        nc.gpsimd.memset(neg_half[:], -0.5)
+        ident_f32 = keep.tile([P, P], F32)
+        make_identity(nc, ident_f32[:])
+        gb_col = keep.tile([P, 2 * FEATURE_TILES], F32)
+        for i, row in enumerate((gamma_raw, beta_raw)):
+            nc.gpsimd.tensor_copy(
+                out=gb_col[:, i * FEATURE_TILES : (i + 1) * FEATURE_TILES], in_=row[:].rearrange("p c t -> p (c t)")
+            )
+
+        wg_codes = keep.tile([P, PASSES, H], U32, align_bytes=64)
+        wg_scales = keep.tile([P, PASSES, H], U8, align_bytes=64)
+        wo_codes = keep.tile([P, PASSES, H], U32, align_bytes=64)
+        wo_scales = keep.tile([P, PASSES, H], U8, align_bytes=64)
+        x_codes = keep.tile([P, PASSES, TOKENS], U32, align_bytes=64)
+        x_scales = keep.tile([P, PASSES, TOKENS], U8, align_bytes=64)
+        h_codes = keep.tile([P, PASSES, TOKENS], U32, align_bytes=64)
+        h_scales = keep.tile([P, PASSES, TOKENS], U8, align_bytes=64)
+
+        def quantise_piece(piece, codes, scales):
+            grouped, c, cols = piece
+            nc.vector.quantize_mx(
+                out=codes[:, c, cols].bitcast(FP8X4),
+                scales=scales[:, c, cols],
+                in_=grouped[:].rearrange("p n j -> p (n j)"),
+            )
+
+        def regroup(grouped, rows):
+            nc.vector.tensor_copy(
+                out=grouped[:].rearrange("p (a i) j -> p a j i", i=4),
+                in_=rows.rearrange("p j (a i) -> p a j i", i=4),
+            )
+
+        def regroup_permuted(grouped, rows):
+            nc.vector.tensor_copy(
+                out=grouped[:].rearrange("p (t m) j -> p t m j", t=PACK),
+                in_=rows.rearrange("p j (m t) -> p t m j", t=PACK),
+            )
+
+        def quantise_weight(raw, codes, scales, lay_out):
+            waiting = None
+            for c in range(PASSES):
+                for first in range(0, H, W_PIECE):
+                    cols = slice(first, first + W_PIECE)
+                    grouped = stage.tile([P, W_PIECE, PACK], BF16, align_bytes=64)
+                    lay_out(grouped, raw[:, c, :, cols])
+                    if waiting is not None:
+                        quantise_piece(waiting, codes, scales)
+                    waiting = (grouped, c, cols)
+            quantise_piece(waiting, codes, scales)
+
+        x_words = x_all[:].bitcast(F32)
+        words_per_tile = H // 2
+        x_grouped = {}
+
+        def transpose_x(ch):
+            grouped = stage.tile([P, PASSES * CHUNK * PACK], BF16, align_bytes=64, name="x_grouped")
+            grouped_words = grouped[:].bitcast(F32).rearrange("p (c t u) -> p c t u", c=PASSES, u=2)
+            for tl, tt in enumerate(chunk_tiles(ch)):
+                xt = psum.tile([P, 2 * PASSES, P], F32, tag="bank")
+                for c in range(PASSES):
+                    for u in range(2):
+                        first = tt * words_per_tile + c * 2 * P
+                        nc.tensor.transpose(
+                            xt[:, 2 * c + u, :], x_words[:, first + u : first + 2 * P : 2], ident_f32[:]
+                        )
+                nc.scalar.copy(
+                    out=grouped_words[:, :, tl * P : (tl + 1) * P, :],
+                    in_=xt[:].rearrange("p (c u) t -> p c t u", u=2),
+                )
+            x_grouped[ch] = grouped
+
+        def quantise_x(ch):
+            toks = slice(ch * CHUNK, (ch + 1) * CHUNK)
+            for c in range(PASSES):
+                nc.vector.quantize_mx(
+                    out=x_codes[:, c, toks].bitcast(FP8X4),
+                    scales=x_scales[:, c, toks],
+                    in_=x_grouped[ch][:, c * CHUNK * PACK : (c + 1) * CHUNK * PACK],
+                )
+
+        z_hat = {}
+        moments = {}
+
+        def take_moments(ch):
+            for tt in chunk_tiles(ch):
+                stats = small.tile([P, H // BN_WIDTH, 6], F32)
+                for a in range(H // BN_WIDTH):
+                    nc.vector.bn_stats(out=stats[:, a, :], in_=z_all[:, tt, a * BN_WIDTH : (a + 1) * BN_WIDTH])
+                mean_var = small.tile([P, 2], F32)
+                nc.vector.bn_aggr(out=mean_var[:], in_=stats[:].rearrange("p a s -> p (a s)"))
+                var_eps = small.tile([P, 1], F32)
+                nc.gpsimd.tensor_scalar(
+                    out=var_eps[:], in0=mean_var[:, 1:2], scalar1=1.0, scalar2=LN_EPS, op0=ALU.mult, op1=ALU.add
+                )
+                rstd = small.tile([P, 1], F32)
+                nc.gpsimd.tensor_tensor(out=rstd[:], in0=var_eps[:], in1=neg_half[:], op=ALU.pow)
+                moments[tt] = (mean_var, rstd)
+
+        def normalise(ch):
+            for tt in chunk_tiles(ch):
+                mean_var, rstd = moments[tt]
+                zh = normed.tile([P, H], F32, name="zh")
+                nc.vector.tensor_scalar(
+                    out=zh[:].rearrange("p (c t m) -> p c t m", c=PASSES, t=PACK),
+                    in0=z_all[:, tt, :].rearrange("p (c m t) -> p c t m", c=PASSES, t=PACK),
+                    scalar1=mean_var[:, 0:1], scalar2=rstd[:],
+                    op0=ALU.subtract, op1=ALU.mult,
+                )
+                z_hat[tt] = zh
+
+        zn_tiles = {}
+
+        def transpose_normed(ch):
+            for c2 in range(PASSES):
+                zn = units.tile([P, PACK, CHUNK], F32)
+                for pair in range(PACK // 2):
+                    zt = psum.tile([P, 2, CHUNK], F32, tag="bank")
+                    for i in range(2):
+                        ft = c2 * PACK + pair * 2 + i
+                        for tl, tt in enumerate(chunk_tiles(ch)):
+                            nc.tensor.transpose(
+                                zt[:, i, tl * P : (tl + 1) * P], z_hat[tt][:, ft * P : (ft + 1) * P], ident_f32[:]
+                            )
+                    for i in range(2):
+                        ft = c2 * PACK + pair * 2 + i
+                        nc.scalar.activation(
+                            out=zn[:, pair * 2 + i, :],
+                            in_=zt[:, i, :],
+                            func=ACT.Identity,
+                            scale=gb_col[:, ft : ft + 1],
+                            bias=gb_col[:, FEATURE_TILES + ft : FEATURE_TILES + ft + 1],
+                        )
+                zn_tiles[(ch, c2)] = zn
+
+        silu_tiles = {}
+
+        def gate_matmul(ch):
+            toks = slice(ch * CHUNK, (ch + 1) * CHUNK)
+            for c2 in range(PASSES):
+                silu_g = units.tile([P, PACK, CHUNK], F32)
+                for pair in range(PACK // 2):
+                    g_bank = psum.tile([P, 2, CHUNK], F32, tag="bank")
+                    for i in range(2):
+                        ft = c2 * PACK + pair * 2 + i
+                        for c in range(PASSES):
+                            nc.tensor.matmul_mx(
+                                out=g_bank[:, i, :],
+                                lhsT=wg_codes[:, c, ft * P : (ft + 1) * P].bitcast(FP8X4),
+                                lhsT_scale=wg_scales[:, c, ft * P : (ft + 1) * P],
+                                rhs=x_codes[:, c, toks].bitcast(FP8X4),
+                                rhs_scale=x_scales[:, c, toks],
+                                start=(c == 0),
+                                stop=(c == PASSES - 1),
+                            )
+                    nc.scalar.activation(out=silu_g[:, pair * 2 : pair * 2 + 2, :], in_=g_bank[:], func=ACT.Silu)
+                silu_tiles[(ch, c2)] = silu_g
+
+        def gate_product(ch, c2):
+            toks = slice(ch * CHUNK, (ch + 1) * CHUNK)
+            h_grouped = stage.tile([P, CHUNK, PACK], BF16, align_bytes=64)
+            nc.vector.tensor_tensor(
+                out=h_grouped[:].rearrange("p (a i) j -> p a j i", i=4),
+                in0=zn_tiles[(ch, c2)][:].rearrange("p j (a i) -> p a j i", i=4),
+                in1=silu_tiles[(ch, c2)][:].rearrange("p j (a i) -> p a j i", i=4),
+                op=ALU.mult,
+            )
+            nc.vector.quantize_mx(
+                out=h_codes[:, c2, toks].bitcast(FP8X4),
+                scales=h_scales[:, c2, toks],
+                in_=h_grouped[:].rearrange("p t j -> p (t j)"),
+            )
+
+        o_banks = {}
+
+        def project_pass(ch, c2):
+            for tt in chunk_tiles(ch):
+                for first in range(0, H, N_OUT):
+                    if c2 == 0:
+                        o_banks[(tt, first)] = psum.tile([P, N_OUT], F32, tag="bank", name="o_bank")
+                    o_bank = o_banks[(tt, first)]
+                    nc.tensor.matmul_mx(
+                        out=o_bank[:],
+                        lhsT=h_codes[:, c2, tt * P : (tt + 1) * P].bitcast(FP8X4),
+                        lhsT_scale=h_scales[:, c2, tt * P : (tt + 1) * P],
+                        rhs=wo_codes[:, c2, first : first + N_OUT].bitcast(FP8X4),
+                        rhs_scale=wo_scales[:, c2, first : first + N_OUT],
+                        start=(c2 == 0),
+                        stop=(c2 == PASSES - 1),
+                    )
+                    if c2 == PASSES - 1:
+                        o_sb = result.tile([P, N_OUT], F32)
+                        nc.scalar.copy(out=o_sb[:], in_=o_bank[:])
+                        nc.sync.dma_start(out=out_dram[tt * P : (tt + 1) * P, first : first + N_OUT], in_=o_sb[:])
+
+        take_moments(0)
+        transpose_x(0)
+        for ch in range(CHUNKS):
+            if ch + 1 < CHUNKS:
+                take_moments(ch + 1)
+                transpose_x(ch + 1)
+            normalise(ch)
+            transpose_normed(ch)
+            quantise_x(ch)
+        quantise_weight(wg_raw, wg_codes, wg_scales, regroup_permuted)
+        for ch in range(CHUNKS):
+            gate_matmul(ch)
+        quantise_weight(wo_raw, wo_codes, wo_scales, regroup)
+        for ch in range(CHUNKS):
+            for c2 in range(PASSES):
+                gate_product(ch, c2)
+                project_pass(ch, c2)

@@ -26,6 +26,8 @@ N_OUT = 512
 LN_EPS = 1e-5
 W_PIECE = 512
 BN_WIDTH = 512
+GPSIMD_TILES = (2, 3)
+VECTOR_BANKS = ((6, 512), (7, 512))
 
 FLOPS = 2 * 2 * TOKENS * H * H
 
@@ -41,58 +43,52 @@ def tile_gatedlinearattention_pb_kernel(tc, z, hidden_states, Wg, Wo, gamma, bet
         keep = ctx.enter_context(tc.tile_pool(name="keep", bufs=1))
         stage = ctx.enter_context(tc.tile_pool(name="stage", bufs=3))
         small = ctx.enter_context(tc.tile_pool(name="small", bufs=TOKEN_TILES))
-        normed = ctx.enter_context(tc.tile_pool(name="normed", bufs=2 * CHUNK_TILES))
+        normed = ctx.enter_context(tc.tile_pool(name="normed", bufs=6))
         units = ctx.enter_context(tc.tile_pool(name="units", bufs=CHUNKS * PASSES))
-        result = ctx.enter_context(tc.tile_pool(name="result", bufs=6))
+        rows = ctx.enter_context(tc.tile_pool(name="rows", bufs=2 * TOKEN_TILES))
         psum = ctx.enter_context(tc.psum_pool(name="psum", bufs=8))
 
         def chunk_tiles(ch):
             return range(ch * CHUNK_TILES, (ch + 1) * CHUNK_TILES)
 
-        z_all = keep.tile([P, TOKEN_TILES, H], BF16)
-        x_all = keep.tile([P, TOKEN_TILES * H], BF16)
+        z_tiles = {}
+        x_tiles = {}
         wg_raw = keep.tile([P, PASSES, PACK, H], BF16)
         wo_raw = keep.tile([P, PASSES, PACK, H], BF16)
-
-        def load_z(ch):
-            first = ch * CHUNK_TILES
-            nc.sync.dma_start(
-                out=z_all[:, first : first + CHUNK_TILES, :],
-                in_=z_dram[ch * CHUNK : (ch + 1) * CHUNK, :].rearrange("(t p) k -> p t k", p=P),
-            )
-
-        def load_x(ch):
-            nc.sync.dma_start(
-                out=x_all[:, ch * CHUNK_TILES * H : (ch + 1) * CHUNK_TILES * H].rearrange("p (t k) -> p t k", k=H),
-                in_=x_dram[ch * CHUNK : (ch + 1) * CHUNK, :].rearrange("(t p) k -> p t k", p=P),
-            )
-
         gamma_raw = keep.tile([P, PASSES, PACK], BF16)
         beta_raw = keep.tile([P, PASSES, PACK], BF16)
 
-        load_z(0)
-        load_x(0)
-        nc.sync.dma_start(out=gamma_raw[:], in_=gamma.rearrange("(c p t) -> p c t", p=P, t=PACK))
-        nc.sync.dma_start(out=beta_raw[:], in_=beta.rearrange("(c p t) -> p c t", p=P, t=PACK))
-        for ch in range(1, CHUNKS):
-            load_z(ch)
-            load_x(ch)
+        def load_rows(tiles, dram, tt):
+            tiles[tt] = rows.tile([P, H], BF16, tag="row", name="row")
+            nc.sync.dma_start(out=tiles[tt][:], in_=dram[tt * P : (tt + 1) * P, :])
+
+        def load_w(raw, w_dram, c):
+            nc.sync.dma_start(
+                out=raw[:, c],
+                in_=w_dram[c * K_PASS : (c + 1) * K_PASS, :].rearrange("(p j) n -> p j n", j=PACK),
+            )
+
+        for tt in range(TOKEN_TILES):
+            load_rows(z_tiles, z_dram, tt)
+            load_rows(x_tiles, x_dram, tt)
+            if tt == 1:
+                nc.sync.dma_start(out=gamma_raw[:], in_=gamma.rearrange("(c p t) -> p c t", p=P, t=PACK))
+                nc.sync.dma_start(out=beta_raw[:], in_=beta.rearrange("(c p t) -> p c t", p=P, t=PACK))
         for raw, w_dram in ((wg_raw, Wg), (wo_raw, Wo)):
             for c in range(PASSES):
-                nc.sync.dma_start(
-                    out=raw[:, c],
-                    in_=w_dram[c * K_PASS : (c + 1) * K_PASS, :].rearrange("(p j) n -> p j n", j=PACK),
-                )
+                load_w(raw, w_dram, c)
 
-        neg_half = keep.tile([P, 1], F32)
+        neg_half = keep.tile([P, CHUNK_TILES], F32)
         nc.gpsimd.memset(neg_half[:], -0.5)
         ident_f32 = keep.tile([P, P], F32)
         make_identity(nc, ident_f32[:])
         gb_col = keep.tile([P, 2 * FEATURE_TILES], F32)
-        for i, row in enumerate((gamma_raw, beta_raw)):
-            nc.gpsimd.tensor_copy(
-                out=gb_col[:, i * FEATURE_TILES : (i + 1) * FEATURE_TILES], in_=row[:].rearrange("p c t -> p (c t)")
-            )
+
+        def spread_gamma_beta():
+            for i, row in enumerate((gamma_raw, beta_raw)):
+                nc.gpsimd.tensor_copy(
+                    out=gb_col[:, i * FEATURE_TILES : (i + 1) * FEATURE_TILES], in_=row[:].rearrange("p c t -> p (c t)")
+                )
 
         wg_codes = keep.tile([P, PASSES, H], U32, align_bytes=64)
         wg_scales = keep.tile([P, PASSES, H], U8, align_bytes=64)
@@ -103,58 +99,52 @@ def tile_gatedlinearattention_pb_kernel(tc, z, hidden_states, Wg, Wo, gamma, bet
         h_codes = keep.tile([P, PASSES, TOKENS], U32, align_bytes=64)
         h_scales = keep.tile([P, PASSES, TOKENS], U8, align_bytes=64)
 
-        def quantise_piece(piece, codes, scales):
-            grouped, c, cols = piece
-            nc.vector.quantize_mx(
-                out=codes[:, c, cols].bitcast(FP8X4),
-                scales=scales[:, c, cols],
-                in_=grouped[:].rearrange("p n j -> p (n j)"),
-            )
-
-        def regroup(grouped, rows):
-            nc.vector.tensor_copy(
+        def regroup_copy(engine_copy, grouped, rows):
+            engine_copy(
                 out=grouped[:].rearrange("p (a i) j -> p a j i", i=4),
                 in_=rows.rearrange("p j (a i) -> p a j i", i=4),
             )
 
-        def regroup_permuted(grouped, rows):
-            nc.vector.tensor_copy(
+        def regroup_permuted(engine_copy, grouped, rows):
+            engine_copy(
                 out=grouped[:].rearrange("p (t m) j -> p t m j", t=PACK),
                 in_=rows.rearrange("p j (m t) -> p t m j", t=PACK),
             )
 
-        def quantise_weight(raw, codes, scales, lay_out):
-            waiting = None
-            for c in range(PASSES):
-                for first in range(0, H, W_PIECE):
-                    cols = slice(first, first + W_PIECE)
-                    grouped = stage.tile([P, W_PIECE, PACK], BF16, align_bytes=64)
-                    lay_out(grouped, raw[:, c, :, cols])
-                    if waiting is not None:
-                        quantise_piece(waiting, codes, scales)
-                    waiting = (grouped, c, cols)
-            quantise_piece(waiting, codes, scales)
+        w_grouped = {}
 
-        x_words = x_all[:].bitcast(F32)
-        words_per_tile = H // 2
+        def regroup_weight(which, c, half, engine_copy):
+            raw, lay_out = {"g": (wg_raw, regroup_permuted), "o": (wo_raw, regroup_copy)}[which]
+            grouped = stage.tile([P, W_PIECE, PACK], BF16, align_bytes=64, name="w_grouped")
+            lay_out(engine_copy, grouped, raw[:, c, :, half * W_PIECE : (half + 1) * W_PIECE])
+            w_grouped[(which, c, half)] = grouped
+
+        def quantise_weight(which, c, half):
+            codes, scales = {"g": (wg_codes, wg_scales), "o": (wo_codes, wo_scales)}[which]
+            cols = slice(half * W_PIECE, (half + 1) * W_PIECE)
+            nc.vector.quantize_mx(
+                out=codes[:, c, cols].bitcast(FP8X4),
+                scales=scales[:, c, cols],
+                in_=w_grouped[(which, c, half)][:].rearrange("p n j -> p (n j)"),
+            )
+
         x_grouped = {}
 
-        def transpose_x(ch):
-            grouped = stage.tile([P, PASSES * CHUNK * PACK], BF16, align_bytes=64, name="x_grouped")
-            grouped_words = grouped[:].bitcast(F32).rearrange("p (c t u) -> p c t u", c=PASSES, u=2)
-            for tl, tt in enumerate(chunk_tiles(ch)):
-                xt = psum.tile([P, 2 * PASSES, P], F32, tag="bank")
-                for c in range(PASSES):
-                    for u in range(2):
-                        first = tt * words_per_tile + c * 2 * P
-                        nc.tensor.transpose(
-                            xt[:, 2 * c + u, :], x_words[:, first + u : first + 2 * P : 2], ident_f32[:]
-                        )
-                nc.scalar.copy(
-                    out=grouped_words[:, :, tl * P : (tl + 1) * P, :],
-                    in_=xt[:].rearrange("p (c u) t -> p c t u", u=2),
-                )
-            x_grouped[ch] = grouped
+        def transpose_x(tt):
+            ch, tl = divmod(tt, CHUNK_TILES)
+            if tl == 0:
+                x_grouped[ch] = stage.tile([P, PASSES * CHUNK * PACK], BF16, align_bytes=64, name="x_grouped")
+            grouped_words = x_grouped[ch][:].bitcast(F32).rearrange("p (c t u) -> p c t u", c=PASSES, u=2)
+            x_words = x_tiles[tt][:].bitcast(F32)
+            xt = psum.tile([P, 2 * PASSES, P], F32, tag="bank")
+            for c in range(PASSES):
+                for u in range(2):
+                    first = c * 2 * P
+                    nc.tensor.transpose(xt[:, 2 * c + u, :], x_words[:, first + u : first + 2 * P : 2], ident_f32[:])
+            nc.scalar.copy(
+                out=grouped_words[:, :, tl * P : (tl + 1) * P, :],
+                in_=xt[:].rearrange("p (c u) t -> p c t u", u=2),
+            )
 
         def quantise_x(ch):
             toks = slice(ch * CHUNK, (ch + 1) * CHUNK)
@@ -166,34 +156,55 @@ def tile_gatedlinearattention_pb_kernel(tc, z, hidden_states, Wg, Wo, gamma, bet
                 )
 
         z_hat = {}
+        stats = {}
         moments = {}
 
-        def take_moments(ch):
-            for tt in chunk_tiles(ch):
-                stats = small.tile([P, H // BN_WIDTH, 6], F32)
-                for a in range(H // BN_WIDTH):
-                    nc.vector.bn_stats(out=stats[:, a, :], in_=z_all[:, tt, a * BN_WIDTH : (a + 1) * BN_WIDTH])
-                mean_var = small.tile([P, 2], F32)
-                nc.vector.bn_aggr(out=mean_var[:], in_=stats[:].rearrange("p a s -> p (a s)"))
-                var_eps = small.tile([P, 1], F32)
-                nc.gpsimd.tensor_scalar(
-                    out=var_eps[:], in0=mean_var[:, 1:2], scalar1=1.0, scalar2=LN_EPS, op0=ALU.mult, op1=ALU.add
-                )
-                rstd = small.tile([P, 1], F32)
-                nc.gpsimd.tensor_tensor(out=rstd[:], in0=var_eps[:], in1=neg_half[:], op=ALU.pow)
-                moments[tt] = (mean_var, rstd)
+        def half_stats(tt, a):
+            if a == 0:
+                stats[tt] = small.tile([P, H // BN_WIDTH, 6], F32, name="stats")
+            nc.vector.bn_stats(out=stats[tt][:, a, :], in_=z_tiles[tt][:, a * BN_WIDTH : (a + 1) * BN_WIDTH])
 
-        def normalise(ch):
-            for tt in chunk_tiles(ch):
-                mean_var, rstd = moments[tt]
-                zh = normed.tile([P, H], F32, name="zh")
+        def finish_stats(tt):
+            ch, tl = divmod(tt, CHUNK_TILES)
+            if tl == 0:
+                moments[ch] = small.tile([P, CHUNK_TILES, 2], F32, name="mean_var")
+            nc.vector.bn_aggr(out=moments[ch][:, tl, :], in_=stats[tt][:].rearrange("p a s -> p (a s)"))
+
+        rstds = {}
+        offsets = {}
+
+        def invert_deviation(ch):
+            var_eps = small.tile([P, CHUNK_TILES], F32)
+            nc.gpsimd.tensor_scalar(
+                out=var_eps[:], in0=moments[ch][:, :, 1], scalar1=1.0, scalar2=LN_EPS, op0=ALU.mult, op1=ALU.add
+            )
+            rstd = small.tile([P, CHUNK_TILES], F32)
+            nc.gpsimd.tensor_tensor(out=rstd[:], in0=var_eps[:], in1=neg_half[:], op=ALU.pow)
+            for tl, tt in enumerate(chunk_tiles(ch)):
+                rstds[tt] = rstd[:, tl : tl + 1]
+                if tt in GPSIMD_TILES:
+                    offset = small.tile([P, 1], F32)
+                    nc.gpsimd.tensor_scalar(
+                        out=offset[:], in0=moments[ch][:, tl, 0:1], scalar1=rstds[tt], scalar2=-1.0,
+                        op0=ALU.mult, op1=ALU.mult,
+                    )
+                    offsets[tt] = offset
+
+        def normalise(tt):
+            ch, tl = divmod(tt, CHUNK_TILES)
+            zh = normed.tile([P, H], F32, name="zh")
+            permuted = zh[:].rearrange("p (c t m) -> p c t m", c=PASSES, t=PACK)
+            z_tile = z_tiles[tt][:].rearrange("p (c m t) -> p c t m", c=PASSES, t=PACK)
+            if tt in GPSIMD_TILES:
+                nc.gpsimd.tensor_scalar(
+                    out=permuted, in0=z_tile, scalar1=rstds[tt], scalar2=offsets[tt][:], op0=ALU.mult, op1=ALU.add
+                )
+            else:
                 nc.vector.tensor_scalar(
-                    out=zh[:].rearrange("p (c t m) -> p c t m", c=PASSES, t=PACK),
-                    in0=z_all[:, tt, :].rearrange("p (c m t) -> p c t m", c=PASSES, t=PACK),
-                    scalar1=mean_var[:, 0:1], scalar2=rstd[:],
+                    out=permuted, in0=z_tile, scalar1=moments[ch][:, tl, 0:1], scalar2=rstds[tt],
                     op0=ALU.subtract, op1=ALU.mult,
                 )
-                z_hat[tt] = zh
+            z_hat[tt] = zh
 
         zn_tiles = {}
 
@@ -221,40 +232,44 @@ def tile_gatedlinearattention_pb_kernel(tc, z, hidden_states, Wg, Wo, gamma, bet
 
         silu_tiles = {}
 
-        def gate_matmul(ch):
+        def gate_matmul(ch, c2):
             toks = slice(ch * CHUNK, (ch + 1) * CHUNK)
-            for c2 in range(PASSES):
-                silu_g = units.tile([P, PACK, CHUNK], F32)
-                for pair in range(PACK // 2):
-                    g_bank = psum.tile([P, 2, CHUNK], F32, tag="bank")
-                    for i in range(2):
-                        ft = c2 * PACK + pair * 2 + i
-                        for c in range(PASSES):
-                            nc.tensor.matmul_mx(
-                                out=g_bank[:, i, :],
-                                lhsT=wg_codes[:, c, ft * P : (ft + 1) * P].bitcast(FP8X4),
-                                lhsT_scale=wg_scales[:, c, ft * P : (ft + 1) * P],
-                                rhs=x_codes[:, c, toks].bitcast(FP8X4),
-                                rhs_scale=x_scales[:, c, toks],
-                                start=(c == 0),
-                                stop=(c == PASSES - 1),
-                            )
-                    nc.scalar.activation(out=silu_g[:, pair * 2 : pair * 2 + 2, :], in_=g_bank[:], func=ACT.Silu)
-                silu_tiles[(ch, c2)] = silu_g
+            silu_g = units.tile([P, PACK, CHUNK], F32)
+            for pair in range(PACK // 2):
+                g_bank = psum.tile([P, 2, CHUNK], F32, tag="bank")
+                for i in range(2):
+                    ft = c2 * PACK + pair * 2 + i
+                    for c in range(PASSES):
+                        nc.tensor.matmul_mx(
+                            out=g_bank[:, i, :],
+                            lhsT=wg_codes[:, c, ft * P : (ft + 1) * P].bitcast(FP8X4),
+                            lhsT_scale=wg_scales[:, c, ft * P : (ft + 1) * P],
+                            rhs=x_codes[:, c, toks].bitcast(FP8X4),
+                            rhs_scale=x_scales[:, c, toks],
+                            start=(c == 0),
+                            stop=(c == PASSES - 1),
+                        )
+                nc.scalar.activation(out=silu_g[:, pair * 2 : pair * 2 + 2, :], in_=g_bank[:], func=ACT.Silu)
+            silu_tiles[(ch, c2)] = silu_g
+
+        h_grouped = {}
 
         def gate_product(ch, c2):
-            toks = slice(ch * CHUNK, (ch + 1) * CHUNK)
-            h_grouped = stage.tile([P, CHUNK, PACK], BF16, align_bytes=64)
+            grouped = stage.tile([P, CHUNK, PACK], BF16, align_bytes=64, name="h_grouped")
             nc.vector.tensor_tensor(
-                out=h_grouped[:].rearrange("p (a i) j -> p a j i", i=4),
+                out=grouped[:].rearrange("p (a i) j -> p a j i", i=4),
                 in0=zn_tiles[(ch, c2)][:].rearrange("p j (a i) -> p a j i", i=4),
                 in1=silu_tiles[(ch, c2)][:].rearrange("p j (a i) -> p a j i", i=4),
                 op=ALU.mult,
             )
+            h_grouped[(ch, c2)] = grouped
+
+        def quantise_h(ch, c2):
+            toks = slice(ch * CHUNK, (ch + 1) * CHUNK)
             nc.vector.quantize_mx(
                 out=h_codes[:, c2, toks].bitcast(FP8X4),
                 scales=h_scales[:, c2, toks],
-                in_=h_grouped[:].rearrange("p t j -> p (t j)"),
+                in_=h_grouped[(ch, c2)][:].rearrange("p t j -> p (t j)"),
             )
 
         o_banks = {}
@@ -275,24 +290,82 @@ def tile_gatedlinearattention_pb_kernel(tc, z, hidden_states, Wg, Wo, gamma, bet
                         stop=(c2 == PASSES - 1),
                     )
                     if c2 == PASSES - 1:
-                        o_sb = result.tile([P, N_OUT], F32)
-                        nc.scalar.copy(out=o_sb[:], in_=o_bank[:])
+                        o_sb = rows.tile([P, N_OUT], F32, tag="row", name="o_sb")
+                        if (tt, first) in VECTOR_BANKS:
+                            nc.vector.tensor_copy(out=o_sb[:], in_=o_bank[:])
+                        else:
+                            nc.scalar.copy(out=o_sb[:], in_=o_bank[:])
                         nc.sync.dma_start(out=out_dram[tt * P : (tt + 1) * P, first : first + N_OUT], in_=o_sb[:])
 
-        take_moments(0)
+        def stats_behind(tt):
+            half_stats(tt, 0)
+            if tt > 0:
+                finish_stats(tt - 1)
+            half_stats(tt, 1)
+
         transpose_x(0)
+        transpose_x(1)
+        spread_gamma_beta()
+        stats_behind(0)
+        stats_behind(1)
+        stats_behind(2)
+        invert_deviation(0)
+        stats_behind(3)
+        normalise(0)
+        normalise(1)
+        transpose_x(2)
+        transpose_x(3)
+        transpose_normed(0)
+        stats_behind(4)
+        invert_deviation(1)
+        normalise(2)
+        normalise(3)
+        transpose_x(4)
+        transpose_x(5)
+        transpose_normed(1)
+        stats_behind(5)
+        stats_behind(6)
+        invert_deviation(2)
+        stats_behind(7)
+        quantise_x(0)
+        finish_stats(7)
+        invert_deviation(3)
+        quantise_x(1)
+        for tt in range(4, TOKEN_TILES):
+            normalise(tt)
+        transpose_x(6)
+        transpose_x(7)
+        transpose_normed(2)
+        transpose_normed(3)
+        for half in range(2):
+            for c in range(PASSES):
+                regroup_weight("g", c, half, nc.vector.tensor_copy)
+            for c in range(PASSES):
+                quantise_weight("g", c, half)
+            if half == 0:
+                quantise_x(2)
+                quantise_x(3)
+            for ch in range(CHUNKS):
+                gate_matmul(ch, half)
+        for half in range(2):
+            regroup_weight("o", 0, half, nc.vector.tensor_copy)
+        regroup_weight("o", 1, 1, nc.scalar.copy)
+        for half in range(2):
+            quantise_weight("o", 0, half)
+        regroup_weight("o", 1, 0, nc.vector.tensor_copy)
+        gate_product(0, 0)
+        quantise_weight("o", 1, 0)
+        gate_product(0, 1)
+        quantise_h(0, 0)
+        project_pass(0, 0)
         for ch in range(CHUNKS):
             if ch + 1 < CHUNKS:
-                take_moments(ch + 1)
-                transpose_x(ch + 1)
-            normalise(ch)
-            transpose_normed(ch)
-            quantise_x(ch)
-        quantise_weight(wg_raw, wg_codes, wg_scales, regroup_permuted)
-        for ch in range(CHUNKS):
-            gate_matmul(ch)
-        quantise_weight(wo_raw, wo_codes, wo_scales, regroup)
-        for ch in range(CHUNKS):
-            for c2 in range(PASSES):
-                gate_product(ch, c2)
-                project_pass(ch, c2)
+                gate_product(ch + 1, 0)
+            if ch == 0:
+                quantise_weight("o", 1, 1)
+            quantise_h(ch, 1)
+            project_pass(ch, 1)
+            if ch + 1 < CHUNKS:
+                gate_product(ch + 1, 1)
+                quantise_h(ch + 1, 0)
+                project_pass(ch + 1, 0)

@@ -24,6 +24,7 @@ CHUNK = CHUNK_TILES * P
 CHUNKS = TOKENS // CHUNK
 N_OUT = 512
 LN_EPS = 1e-5
+RUN = 4
 W_PIECE = 512
 BN_WIDTH = 512
 GPSIMD_TILES = (2, 3)
@@ -43,7 +44,7 @@ def tile_gatedlinearattention_pb_kernel(tc, z, hidden_states, Wg, Wo, gamma, bet
         keep = ctx.enter_context(tc.tile_pool(name="keep", bufs=1))
         stage = ctx.enter_context(tc.tile_pool(name="stage", bufs=3))
         small = ctx.enter_context(tc.tile_pool(name="small", bufs=TOKEN_TILES))
-        normed = ctx.enter_context(tc.tile_pool(name="normed", bufs=6))
+        normed = ctx.enter_context(tc.tile_pool(name="normed", bufs=TOKEN_TILES))
         units = ctx.enter_context(tc.tile_pool(name="units", bufs=CHUNKS * PASSES))
         rows = ctx.enter_context(tc.tile_pool(name="rows", bufs=2 * TOKEN_TILES))
         psum = ctx.enter_context(tc.psum_pool(name="psum", bufs=8))
@@ -53,42 +54,67 @@ def tile_gatedlinearattention_pb_kernel(tc, z, hidden_states, Wg, Wo, gamma, bet
 
         z_tiles = {}
         x_tiles = {}
-        wg_raw = keep.tile([P, PASSES, PACK, H], BF16)
-        wo_raw = keep.tile([P, PASSES, PACK, H], BF16)
-        gamma_raw = keep.tile([P, PASSES, PACK], BF16)
-        beta_raw = keep.tile([P, PASSES, PACK], BF16)
+        w_raw = {}
+        gb_rows = {}
+        for which in ("gamma", "beta"):
+            gb_rows[which] = keep.tile([P, P], BF16, name="rows_" + which)
+            nc.gpsimd.memset(gb_rows[which][:], 0.0)
 
         def load_rows(tiles, dram, tt):
             tiles[tt] = rows.tile([P, H], BF16, tag="row", name="row")
             nc.sync.dma_start(out=tiles[tt][:], in_=dram[tt * P : (tt + 1) * P, :])
 
-        def load_w(raw, w_dram, c):
-            nc.sync.dma_start(
-                out=raw[:, c],
-                in_=w_dram[c * K_PASS : (c + 1) * K_PASS, :].rearrange("(p j) n -> p j n", j=PACK),
-            )
+        def load_w(which, w_dram, c, half):
+            raw = keep.tile([P, PACK, W_PIECE], BF16, name="w_raw_%s%d%d" % (which, c, half))
+            piece = w_dram[c * K_PASS : (c + 1) * K_PASS, half * W_PIECE : (half + 1) * W_PIECE]
+            if which == "g":
+                nc.sync.dma_start(out=raw[:], in_=piece.rearrange("(p j) n -> p j n", j=PACK))
+            else:
+                for i in range(RUN):
+                    nc.sync.dma_start(
+                        out=raw[i:P:RUN],
+                        in_=piece.rearrange("(a j i) n -> i a j n", j=PACK, i=RUN)[i],
+                    )
+            w_raw[(which, c, half)] = raw
 
+        load_w("g", Wg, 0, 0)
+        load_rows(x_tiles, x_dram, 0)
+        load_w("g", Wg, 1, 0)
+        for tt in (1, 2, 3):
+            load_rows(x_tiles, x_dram, tt)
+        for c in range(PASSES):
+            load_w("g", Wg, c, 1)
+            for tt in (2 * c + 4, 2 * c + 5):
+                load_rows(x_tiles, x_dram, tt)
         for tt in range(TOKEN_TILES):
             load_rows(z_tiles, z_dram, tt)
-            load_rows(x_tiles, x_dram, tt)
             if tt == 1:
-                nc.sync.dma_start(out=gamma_raw[:], in_=gamma.rearrange("(c p t) -> p c t", p=P, t=PACK))
-                nc.sync.dma_start(out=beta_raw[:], in_=beta.rearrange("(c p t) -> p c t", p=P, t=PACK))
-        for raw, w_dram in ((wg_raw, Wg), (wo_raw, Wo)):
-            for c in range(PASSES):
-                load_w(raw, w_dram, c)
+                for which, dram in (("gamma", gamma), ("beta", beta)):
+                    for c in range(PASSES):
+                        nc.sync.dma_start(
+                            out=gb_rows[which][c * PACK : (c + 1) * PACK, :].rearrange("t (a i) -> t a i", i=RUN),
+                            in_=dram[c * K_PASS : (c + 1) * K_PASS].rearrange("(a t i) -> t a i", t=PACK, i=RUN),
+                        )
+        for c in range(PASSES):
+            for half in range(2):
+                load_w("o", Wo, c, half)
 
         neg_half = keep.tile([P, CHUNK_TILES], F32)
         nc.gpsimd.memset(neg_half[:], -0.5)
+        warm = keep.tile([P, 1], F32)
+        nc.scalar.activation(out=warm[:], in_=neg_half[:, 0:1], func=ACT.Silu)
         ident_f32 = keep.tile([P, P], F32)
         make_identity(nc, ident_f32[:])
-        gb_col = keep.tile([P, 2 * FEATURE_TILES], F32)
+        ident_bf16 = keep.tile([P, P], BF16)
+        make_identity(nc, ident_bf16[:])
+        gb_col = {}
 
         def spread_gamma_beta():
-            for i, row in enumerate((gamma_raw, beta_raw)):
-                nc.gpsimd.tensor_copy(
-                    out=gb_col[:, i * FEATURE_TILES : (i + 1) * FEATURE_TILES], in_=row[:].rearrange("p c t -> p (c t)")
-                )
+            for which in ("gamma", "beta"):
+                gb_t = psum.tile([P, P], BF16, tag="bank")
+                nc.tensor.transpose(gb_t[:], gb_rows[which][:], ident_bf16[:])
+                gb_col[which] = keep.tile([P, FEATURE_TILES], F32, name="col_" + which)
+                nc.scalar.copy(out=gb_col[which][:], in_=gb_t[:, 0:FEATURE_TILES])
 
         wg_codes = keep.tile([P, PASSES, H], U32, align_bytes=64)
         wg_scales = keep.tile([P, PASSES, H], U8, align_bytes=64)
@@ -106,17 +132,18 @@ def tile_gatedlinearattention_pb_kernel(tc, z, hidden_states, Wg, Wo, gamma, bet
             )
 
         def regroup_permuted(engine_copy, grouped, rows):
-            engine_copy(
-                out=grouped[:].rearrange("p (t m) j -> p t m j", t=PACK),
-                in_=rows.rearrange("p j (m t) -> p t m j", t=PACK),
-            )
+            for t in range(PACK):
+                engine_copy(
+                    out=grouped[:, t * P : (t + 1) * P, :].rearrange("p (a i) j -> p a j i", i=RUN),
+                    in_=rows.rearrange("p j (a t i) -> p t a j i", t=PACK, i=RUN)[:, t],
+                )
 
         w_grouped = {}
 
         def regroup_weight(which, c, half, engine_copy):
-            raw, lay_out = {"g": (wg_raw, regroup_permuted), "o": (wo_raw, regroup_copy)}[which]
+            lay_out = {"g": regroup_permuted, "o": regroup_copy}[which]
             grouped = stage.tile([P, W_PIECE, PACK], BF16, align_bytes=64, name="w_grouped")
-            lay_out(engine_copy, grouped, raw[:, c, :, half * W_PIECE : (half + 1) * W_PIECE])
+            lay_out(engine_copy, grouped, w_raw[(which, c, half)][:])
             w_grouped[(which, c, half)] = grouped
 
         def quantise_weight(which, c, half):
@@ -193,8 +220,8 @@ def tile_gatedlinearattention_pb_kernel(tc, z, hidden_states, Wg, Wo, gamma, bet
         def normalise(tt):
             ch, tl = divmod(tt, CHUNK_TILES)
             zh = normed.tile([P, H], F32, name="zh")
-            permuted = zh[:].rearrange("p (c t m) -> p c t m", c=PASSES, t=PACK)
-            z_tile = z_tiles[tt][:].rearrange("p (c m t) -> p c t m", c=PASSES, t=PACK)
+            permuted = zh[:].rearrange("p (t a i) -> p t a i", t=PACK, i=RUN)
+            z_tile = z_tiles[tt][:].rearrange("p (a t i) -> p t a i", t=PACK, i=RUN)
             if tt in GPSIMD_TILES:
                 nc.gpsimd.tensor_scalar(
                     out=permuted, in0=z_tile, scalar1=rstds[tt], scalar2=offsets[tt][:], op0=ALU.mult, op1=ALU.add
@@ -214,10 +241,10 @@ def tile_gatedlinearattention_pb_kernel(tc, z, hidden_states, Wg, Wo, gamma, bet
                 for pair in range(PACK // 2):
                     zt = psum.tile([P, 2, CHUNK], F32, tag="bank")
                     for i in range(2):
-                        ft = c2 * PACK + pair * 2 + i
+                        first = (pair * 2 + i) * PASSES * P + c2 * P
                         for tl, tt in enumerate(chunk_tiles(ch)):
                             nc.tensor.transpose(
-                                zt[:, i, tl * P : (tl + 1) * P], z_hat[tt][:, ft * P : (ft + 1) * P], ident_f32[:]
+                                zt[:, i, tl * P : (tl + 1) * P], z_hat[tt][:, first : first + P], ident_f32[:]
                             )
                     for i in range(2):
                         ft = c2 * PACK + pair * 2 + i
@@ -225,8 +252,8 @@ def tile_gatedlinearattention_pb_kernel(tc, z, hidden_states, Wg, Wo, gamma, bet
                             out=zn[:, pair * 2 + i, :],
                             in_=zt[:, i, :],
                             func=ACT.Identity,
-                            scale=gb_col[:, ft : ft + 1],
-                            bias=gb_col[:, FEATURE_TILES + ft : FEATURE_TILES + ft + 1],
+                            scale=gb_col["gamma"][:, ft : ft + 1],
+                            bias=gb_col["beta"][:, ft : ft + 1],
                         )
                 zn_tiles[(ch, c2)] = zn
 
@@ -297,59 +324,45 @@ def tile_gatedlinearattention_pb_kernel(tc, z, hidden_states, Wg, Wo, gamma, bet
                             nc.scalar.copy(out=o_sb[:], in_=o_bank[:])
                         nc.sync.dma_start(out=out_dram[tt * P : (tt + 1) * P, first : first + N_OUT], in_=o_sb[:])
 
-        def stats_behind(tt):
-            half_stats(tt, 0)
-            if tt > 0:
-                finish_stats(tt - 1)
-            half_stats(tt, 1)
-
-        transpose_x(0)
-        transpose_x(1)
-        spread_gamma_beta()
-        stats_behind(0)
-        stats_behind(1)
-        stats_behind(2)
-        invert_deviation(0)
-        stats_behind(3)
-        normalise(0)
-        normalise(1)
-        transpose_x(2)
-        transpose_x(3)
-        transpose_normed(0)
-        stats_behind(4)
-        invert_deviation(1)
-        normalise(2)
-        normalise(3)
-        transpose_x(4)
-        transpose_x(5)
-        transpose_normed(1)
-        stats_behind(5)
-        stats_behind(6)
-        invert_deviation(2)
-        stats_behind(7)
-        quantise_x(0)
-        finish_stats(7)
-        invert_deviation(3)
-        quantise_x(1)
-        for tt in range(4, TOKEN_TILES):
-            normalise(tt)
-        transpose_x(6)
-        transpose_x(7)
-        transpose_normed(2)
-        transpose_normed(3)
         for half in range(2):
             for c in range(PASSES):
                 regroup_weight("g", c, half, nc.vector.tensor_copy)
+            for tt in ((0, 1, 2, 3, 4, 5), (6, 7))[half]:
+                transpose_x(tt)
             for c in range(PASSES):
                 quantise_weight("g", c, half)
-            if half == 0:
-                quantise_x(2)
-                quantise_x(3)
-            for ch in range(CHUNKS):
-                gate_matmul(ch, half)
-        for half in range(2):
-            regroup_weight("o", 0, half, nc.vector.tensor_copy)
+            for ch in range(2 * half, 2 * half + 2):
+                quantise_x(ch)
+            for ch in range(2 * half, 2 * half + 2):
+                gate_matmul(ch, 0)
+        for ch in range(CHUNKS):
+            gate_matmul(ch, 1)
+
+        spread_gamma_beta()
+        for tt in range(TOKEN_TILES):
+            half_stats(tt, 0)
+            if tt > 0:
+                finish_stats(tt - 1)
+            if tt in (2, 4, 6):
+                invert_deviation(tt // 2 - 1)
+                for t in chunk_tiles(tt // 2 - 1):
+                    if t in GPSIMD_TILES:
+                        normalise(t)
+            half_stats(tt, 1)
+            if tt == 3:
+                normalise(0)
+                normalise(1)
+                transpose_normed(0)
+        transpose_normed(1)
+        regroup_weight("o", 0, 0, nc.vector.tensor_copy)
+        finish_stats(TOKEN_TILES - 1)
+        invert_deviation(CHUNKS - 1)
+        for tt in range(4, TOKEN_TILES):
+            normalise(tt)
+        transpose_normed(2)
+        transpose_normed(3)
         regroup_weight("o", 1, 1, nc.scalar.copy)
+        regroup_weight("o", 0, 1, nc.vector.tensor_copy)
         for half in range(2):
             quantise_weight("o", 0, half)
         regroup_weight("o", 1, 0, nc.vector.tensor_copy)

@@ -22,13 +22,14 @@ FEATURE_TILES = H // P
 CHUNK_TILES = 2
 CHUNK = CHUNK_TILES * P
 CHUNKS = TOKENS // CHUNK
+VECTOR_BANKS = ((7, 512),)
+TILE_SLICES = tuple(slice(tl * P, (tl + 1) * P) for tl in range(CHUNK_TILES))
 N_OUT = 512
 LN_EPS = 1e-5
 RUN = 4
 W_PIECE = 512
 BN_WIDTH = 512
 GPSIMD_TILES = (2, 3)
-VECTOR_BANKS = ((6, 512), (7, 512))
 
 FLOPS = 2 * 2 * TOKENS * H * H
 
@@ -80,13 +81,16 @@ def tile_gatedlinearattention_pb_kernel(tc, z, hidden_states, Wg, Wo, gamma, bet
         load_w("g", Wg, 0, 0)
         load_rows(x_tiles, x_dram, 0)
         load_w("g", Wg, 1, 0)
-        for tt in (1, 2, 3):
+        load_rows(x_tiles, x_dram, 1)
+        load_rows(x_tiles, x_dram, 2)
+        load_w("g", Wg, 1, 1)
+        load_rows(x_tiles, x_dram, 3)
+        load_w("g", Wg, 0, 1)
+        load_rows(x_tiles, x_dram, 4)
+        load_rows(z_tiles, z_dram, 0)
+        for tt in range(5, TOKEN_TILES):
             load_rows(x_tiles, x_dram, tt)
-        for c in range(PASSES):
-            load_w("g", Wg, c, 1)
-            for tt in (2 * c + 4, 2 * c + 5):
-                load_rows(x_tiles, x_dram, tt)
-        for tt in range(TOKEN_TILES):
+        for tt in range(1, TOKEN_TILES):
             load_rows(z_tiles, z_dram, tt)
             if tt == 1:
                 for which, dram in (("gamma", gamma), ("beta", beta)):
@@ -131,8 +135,8 @@ def tile_gatedlinearattention_pb_kernel(tc, z, hidden_states, Wg, Wo, gamma, bet
                 in_=rows.rearrange("p j (a i) -> p a j i", i=4),
             )
 
-        def regroup_permuted(engine_copy, grouped, rows):
-            for t in range(PACK):
+        def regroup_permuted(engine_copy, grouped, rows, parts=range(PACK)):
+            for t in parts:
                 engine_copy(
                     out=grouped[:, t * P : (t + 1) * P, :].rearrange("p (a i) j -> p a j i", i=RUN),
                     in_=rows.rearrange("p j (a t i) -> p t a j i", t=PACK, i=RUN)[:, t],
@@ -281,34 +285,33 @@ def tile_gatedlinearattention_pb_kernel(tc, z, hidden_states, Wg, Wo, gamma, bet
 
         h_grouped = {}
 
-        def gate_product(ch, c2):
-            grouped = stage.tile([P, CHUNK, PACK], BF16, align_bytes=64, name="h_grouped")
+        def gate_product(ch, c2, toks=slice(0, CHUNK)):
+            grouped = stage.tile([P, toks.stop - toks.start, PACK], BF16, align_bytes=64, name="h_grouped")
             nc.vector.tensor_tensor(
                 out=grouped[:].rearrange("p (a i) j -> p a j i", i=4),
-                in0=zn_tiles[(ch, c2)][:].rearrange("p j (a i) -> p a j i", i=4),
-                in1=silu_tiles[(ch, c2)][:].rearrange("p j (a i) -> p a j i", i=4),
+                in0=zn_tiles[(ch, c2)][:, :, toks].rearrange("p j (a i) -> p a j i", i=4),
+                in1=silu_tiles[(ch, c2)][:, :, toks].rearrange("p j (a i) -> p a j i", i=4),
                 op=ALU.mult,
             )
-            h_grouped[(ch, c2)] = grouped
+            h_grouped[(ch, c2, toks.start)] = grouped
 
-        def quantise_h(ch, c2):
-            toks = slice(ch * CHUNK, (ch + 1) * CHUNK)
+        def quantise_h(ch, c2, toks=slice(0, CHUNK)):
+            all_toks = slice(ch * CHUNK + toks.start, ch * CHUNK + toks.stop)
             nc.vector.quantize_mx(
-                out=h_codes[:, c2, toks].bitcast(FP8X4),
-                scales=h_scales[:, c2, toks],
-                in_=h_grouped[(ch, c2)][:].rearrange("p t j -> p (t j)"),
+                out=h_codes[:, c2, all_toks].bitcast(FP8X4),
+                scales=h_scales[:, c2, all_toks],
+                in_=h_grouped[(ch, c2, toks.start)][:].rearrange("p t j -> p (t j)"),
             )
 
         o_banks = {}
 
-        def project_pass(ch, c2):
-            for tt in chunk_tiles(ch):
+        def project_pass(c2, tiles):
+            for tt in tiles:
                 for first in range(0, H, N_OUT):
                     if c2 == 0:
                         o_banks[(tt, first)] = psum.tile([P, N_OUT], F32, tag="bank", name="o_bank")
-                    o_bank = o_banks[(tt, first)]
                     nc.tensor.matmul_mx(
-                        out=o_bank[:],
+                        out=o_banks[(tt, first)][:],
                         lhsT=h_codes[:, c2, tt * P : (tt + 1) * P].bitcast(FP8X4),
                         lhsT_scale=h_scales[:, c2, tt * P : (tt + 1) * P],
                         rhs=wo_codes[:, c2, first : first + N_OUT].bitcast(FP8X4),
@@ -316,69 +319,89 @@ def tile_gatedlinearattention_pb_kernel(tc, z, hidden_states, Wg, Wo, gamma, bet
                         start=(c2 == 0),
                         stop=(c2 == PASSES - 1),
                     )
-                    if c2 == PASSES - 1:
-                        o_sb = rows.tile([P, N_OUT], F32, tag="row", name="o_sb")
-                        if (tt, first) in VECTOR_BANKS:
-                            nc.vector.tensor_copy(out=o_sb[:], in_=o_bank[:])
-                        else:
-                            nc.scalar.copy(out=o_sb[:], in_=o_bank[:])
-                        nc.sync.dma_start(out=out_dram[tt * P : (tt + 1) * P, first : first + N_OUT], in_=o_sb[:])
 
-        for half in range(2):
-            for c in range(PASSES):
-                regroup_weight("g", c, half, nc.vector.tensor_copy)
-            for tt in ((0, 1, 2, 3, 4, 5), (6, 7))[half]:
-                transpose_x(tt)
-            for c in range(PASSES):
-                quantise_weight("g", c, half)
-            for ch in range(2 * half, 2 * half + 2):
-                quantise_x(ch)
-            for ch in range(2 * half, 2 * half + 2):
-                gate_matmul(ch, 0)
-        for ch in range(CHUNKS):
-            gate_matmul(ch, 1)
+        def drain(tt, first, engine_copy):
+            o_sb = rows.tile([P, N_OUT], F32, tag="row", name="o_sb")
+            engine_copy(out=o_sb[:], in_=o_banks[(tt, first)][:])
+            nc.sync.dma_start(out=out_dram[tt * P : (tt + 1) * P, first : first + N_OUT], in_=o_sb[:])
 
-        spread_gamma_beta()
+        for c in range(PASSES):
+            regroup_weight("g", c, 0, nc.vector.tensor_copy)
+            transpose_x(c)
+        for c in range(PASSES):
+            quantise_weight("g", c, 0)
+        regroup_weight("g", 1, 1, nc.vector.tensor_copy)
+        w_grouped[("g", 0, 1)] = stage.tile([P, W_PIECE, PACK], BF16, align_bytes=64, name="w_grouped")
+        for t in range(PACK):
+            regroup_permuted(nc.scalar.copy, w_grouped[("g", 0, 1)], w_raw[("g", 0, 1)][:], (t,))
+            transpose_x(2 + t)
+        quantise_weight("g", 1, 1)
+        quantise_x(0)
+        half_stats(0, 0)
+        half_stats(0, 1)
+        quantise_x(1)
+        quantise_weight("g", 0, 1)
+        gate_matmul(0, 0)
+        transpose_x(6)
+        transpose_x(7)
+        gate_matmul(1, 0)
+        quantise_x(2)
+        gate_matmul(2, 0)
+
+        def vector_normalise(ch):
+            for tt in chunk_tiles(ch):
+                if tt not in GPSIMD_TILES:
+                    normalise(tt)
+
         for tt in range(TOKEN_TILES):
-            half_stats(tt, 0)
             if tt > 0:
+                half_stats(tt, 0)
                 finish_stats(tt - 1)
             if tt in (2, 4, 6):
                 invert_deviation(tt // 2 - 1)
                 for t in chunk_tiles(tt // 2 - 1):
                     if t in GPSIMD_TILES:
                         normalise(t)
-            half_stats(tt, 1)
-            if tt == 3:
-                normalise(0)
-                normalise(1)
-                transpose_normed(0)
-        transpose_normed(1)
+            if tt > 0:
+                half_stats(tt, 1)
+            if tt == 1:
+                quantise_x(3)
+                gate_matmul(3, 0)
+                for ch in range(CHUNKS):
+                    gate_matmul(ch, 1)
+                spread_gamma_beta()
+            if tt in (4, 6):
+                vector_normalise(tt // 2 - 2)
+                transpose_normed(tt // 2 - 2)
         regroup_weight("o", 0, 0, nc.vector.tensor_copy)
         finish_stats(TOKEN_TILES - 1)
         invert_deviation(CHUNKS - 1)
-        for tt in range(4, TOKEN_TILES):
-            normalise(tt)
+        vector_normalise(2)
         transpose_normed(2)
-        transpose_normed(3)
-        regroup_weight("o", 1, 1, nc.scalar.copy)
         regroup_weight("o", 0, 1, nc.vector.tensor_copy)
+        regroup_weight("o", 1, 1, nc.scalar.copy)
+        vector_normalise(3)
+        transpose_normed(3)
         for half in range(2):
             quantise_weight("o", 0, half)
         regroup_weight("o", 1, 0, nc.vector.tensor_copy)
-        gate_product(0, 0)
-        quantise_weight("o", 1, 0)
-        gate_product(0, 1)
-        quantise_h(0, 0)
-        project_pass(0, 0)
+        WHOLE = slice(0, CHUNK)
+        steps = []
         for ch in range(CHUNKS):
-            if ch + 1 < CHUNKS:
-                gate_product(ch + 1, 0)
-            if ch == 0:
+            for toks in ((WHOLE,) if ch < 2 else TILE_SLICES):
+                for c2 in range(PASSES):
+                    steps.append((ch, c2, toks))
+        gate_product(*steps[0])
+        quantise_weight("o", 1, 0)
+        for i, (ch, c2, toks) in enumerate(steps):
+            if i + 1 < len(steps):
+                gate_product(*steps[i + 1])
+            if i == 1:
                 quantise_weight("o", 1, 1)
-            quantise_h(ch, 1)
-            project_pass(ch, 1)
-            if ch + 1 < CHUNKS:
-                gate_product(ch + 1, 1)
-                quantise_h(ch + 1, 0)
-                project_pass(ch + 1, 0)
+            quantise_h(ch, c2, toks)
+            tiles = [ch * CHUNK_TILES + t for t in range(toks.start // P, toks.stop // P)]
+            project_pass(c2, tiles)
+            if c2 == PASSES - 1:
+                for tt in tiles:
+                    for first in range(0, H, N_OUT):
+                        drain(tt, first, nc.vector.tensor_copy if (tt, first) in VECTOR_BANKS else nc.scalar.copy)

@@ -29,7 +29,7 @@ LN_EPS = 1e-5
 RUN = 4
 W_PIECE = 512
 BN_WIDTH = 512
-GPSIMD_TILES = (2, 3)
+GPSIMD_TILES = ()
 
 FLOPS = 2 * 2 * TOKENS * H * H
 

@@ -13,6 +13,7 @@ ACT = mybir.ActivationFunctionType
 
 P = 128
 PACK = 4
+RUN = 4
 K_PASS = P * PACK
 TOKENS = 1024
 H = 1024
@@ -22,32 +23,28 @@ FEATURE_TILES = H // P
 CHUNK_TILES = 2
 CHUNK = CHUNK_TILES * P
 CHUNKS = TOKENS // CHUNK
-VECTOR_BANKS = ((7, 512),)
-TILE_SLICES = tuple(slice(tl * P, (tl + 1) * P) for tl in range(CHUNK_TILES))
 N_OUT = 512
 LN_EPS = 1e-5
-RUN = 4
-W_PIECE = 512
+SCALAR_TILES = (1,)
 BN_WIDTH = 512
-GPSIMD_TILES = ()
 
 FLOPS = 2 * 2 * TOKENS * H * H
 
 
 def tile_gatedlinearattention_pb_kernel(tc, z, hidden_states, Wg, Wo, gamma, beta, out):
     nc = tc.nc
-    x_dram = hidden_states.flatten_outer_dims()
-    z_dram = z.flatten_outer_dims()
-    out_dram = out.flatten_outer_dims()
+    x_dram = hidden_states.flatten_outer_dims().rearrange("(p t) k -> p t k", t=TOKEN_TILES)
+    z_dram = z.flatten_outer_dims().rearrange("(p t) k -> p t k", t=TOKEN_TILES)
+    out_dram = out.flatten_outer_dims().rearrange("(p t) m -> p t m", t=TOKEN_TILES)
 
     with ExitStack() as ctx:
         ctx.enter_context(tc.manual_schedule())
         keep = ctx.enter_context(tc.tile_pool(name="keep", bufs=1))
-        stage = ctx.enter_context(tc.tile_pool(name="stage", bufs=3))
+        stage = ctx.enter_context(tc.tile_pool(name="stage", bufs=2))
         small = ctx.enter_context(tc.tile_pool(name="small", bufs=TOKEN_TILES))
-        normed = ctx.enter_context(tc.tile_pool(name="normed", bufs=TOKEN_TILES))
-        units = ctx.enter_context(tc.tile_pool(name="units", bufs=CHUNKS * PASSES))
-        rows = ctx.enter_context(tc.tile_pool(name="rows", bufs=2 * TOKEN_TILES))
+        normed = ctx.enter_context(tc.tile_pool(name="normed", bufs=6))
+        units = ctx.enter_context(tc.tile_pool(name="units", bufs=CHUNKS))
+        rows = ctx.enter_context(tc.tile_pool(name="rows", bufs=2 * CHUNKS + 1))
         psum = ctx.enter_context(tc.psum_pool(name="psum", bufs=8))
 
         def chunk_tiles(ch):
@@ -61,13 +58,19 @@ def tile_gatedlinearattention_pb_kernel(tc, z, hidden_states, Wg, Wo, gamma, bet
             gb_rows[which] = keep.tile([P, P], BF16, name="rows_" + which)
             nc.gpsimd.memset(gb_rows[which][:], 0.0)
 
-        def load_rows(tiles, dram, tt):
-            tiles[tt] = rows.tile([P, H], BF16, tag="row", name="row")
-            nc.sync.dma_start(out=tiles[tt][:], in_=dram[tt * P : (tt + 1) * P, :])
+        def load_chunk(tiles, dram, ch):
+            chunk = rows.tile([P, CHUNK_TILES, H], BF16, tag="row", name="row")
+            nc.sync.dma_start(out=chunk[:], in_=dram[:, ch * CHUNK_TILES : (ch + 1) * CHUNK_TILES, :])
+            for tl, tt in enumerate(chunk_tiles(ch)):
+                tiles[tt] = chunk[:, tl, :]
 
-        def load_w(which, w_dram, c, half):
-            raw = keep.tile([P, PACK, W_PIECE], BF16, name="w_raw_%s%d%d" % (which, c, half))
-            piece = w_dram[c * K_PASS : (c + 1) * K_PASS, half * W_PIECE : (half + 1) * W_PIECE]
+        def load_row(tiles, dram, tt):
+            tiles[tt] = rows.tile([P, H], BF16, tag="row", name="row")[:]
+            nc.sync.dma_start(out=tiles[tt], in_=dram[:, tt, :])
+
+        def load_w(which, w_dram, c):
+            raw = keep.tile([P, PACK, H], BF16, name="w_raw_%s%d" % (which, c))
+            piece = w_dram[c * K_PASS : (c + 1) * K_PASS, :]
             if which == "g":
                 nc.sync.dma_start(out=raw[:], in_=piece.rearrange("(p j) n -> p j n", j=PACK))
             else:
@@ -76,32 +79,30 @@ def tile_gatedlinearattention_pb_kernel(tc, z, hidden_states, Wg, Wo, gamma, bet
                         out=raw[i:P:RUN],
                         in_=piece.rearrange("(a j i) n -> i a j n", j=PACK, i=RUN)[i],
                     )
-            w_raw[(which, c, half)] = raw
+            w_raw[(which, c)] = raw
 
-        load_w("g", Wg, 0, 0)
-        load_rows(x_tiles, x_dram, 0)
-        load_w("g", Wg, 1, 0)
-        load_rows(x_tiles, x_dram, 1)
-        load_rows(x_tiles, x_dram, 2)
-        load_w("g", Wg, 1, 1)
-        load_rows(x_tiles, x_dram, 3)
-        load_w("g", Wg, 0, 1)
-        load_rows(x_tiles, x_dram, 4)
-        load_rows(z_tiles, z_dram, 0)
-        for tt in range(5, TOKEN_TILES):
-            load_rows(x_tiles, x_dram, tt)
-        for tt in range(1, TOKEN_TILES):
-            load_rows(z_tiles, z_dram, tt)
-            if tt == 1:
-                for which, dram in (("gamma", gamma), ("beta", beta)):
-                    for c in range(PASSES):
-                        nc.sync.dma_start(
-                            out=gb_rows[which][c * PACK : (c + 1) * PACK, :].rearrange("t (a i) -> t a i", i=RUN),
-                            in_=dram[c * K_PASS : (c + 1) * K_PASS].rearrange("(a t i) -> t a i", t=PACK, i=RUN),
-                        )
+        def load_gamma_beta():
+            for which, dram in (("gamma", gamma), ("beta", beta)):
+                for c in range(PASSES):
+                    nc.sync.dma_start(
+                        out=gb_rows[which][c * PACK : (c + 1) * PACK, :].rearrange("t (a i) -> t a i", i=RUN),
+                        in_=dram[c * K_PASS : (c + 1) * K_PASS].rearrange("(a t i) -> t a i", t=PACK, i=RUN),
+                    )
+
+        load_row(z_tiles, z_dram, 0)
+        load_row(z_tiles, z_dram, 1)
+        load_chunk(x_tiles, x_dram, 0)
+        load_chunk(z_tiles, z_dram, 1)
+        load_chunk(x_tiles, x_dram, 1)
+        load_gamma_beta()
+        load_chunk(z_tiles, z_dram, 2)
+        load_chunk(z_tiles, z_dram, 3)
+        load_w("g", Wg, 0)
+        load_chunk(x_tiles, x_dram, 2)
+        load_w("g", Wg, 1)
+        load_chunk(x_tiles, x_dram, 3)
         for c in range(PASSES):
-            for half in range(2):
-                load_w("o", Wo, c, half)
+            load_w("o", Wo, c)
 
         neg_half = keep.tile([P, CHUNK_TILES], F32)
         nc.gpsimd.memset(neg_half[:], -0.5)
@@ -120,75 +121,71 @@ def tile_gatedlinearattention_pb_kernel(tc, z, hidden_states, Wg, Wo, gamma, bet
                 gb_col[which] = keep.tile([P, FEATURE_TILES], F32, name="col_" + which)
                 nc.scalar.copy(out=gb_col[which][:], in_=gb_t[:, 0:FEATURE_TILES])
 
-        wg_codes = keep.tile([P, PASSES, H], U32, align_bytes=64)
-        wg_scales = keep.tile([P, PASSES, H], U8, align_bytes=64)
-        wo_codes = keep.tile([P, PASSES, H], U32, align_bytes=64)
-        wo_scales = keep.tile([P, PASSES, H], U8, align_bytes=64)
-        x_codes = keep.tile([P, PASSES, TOKENS], U32, align_bytes=64)
-        x_scales = keep.tile([P, PASSES, TOKENS], U8, align_bytes=64)
-        h_codes = keep.tile([P, PASSES, TOKENS], U32, align_bytes=64)
-        h_scales = keep.tile([P, PASSES, TOKENS], U8, align_bytes=64)
-
-        def regroup_copy(engine_copy, grouped, rows):
-            engine_copy(
-                out=grouped[:].rearrange("p (a i) j -> p a j i", i=4),
-                in_=rows.rearrange("p j (a i) -> p a j i", i=4),
-            )
-
-        def regroup_permuted(engine_copy, grouped, rows, parts=range(PACK)):
-            for t in parts:
-                engine_copy(
-                    out=grouped[:, t * P : (t + 1) * P, :].rearrange("p (a i) j -> p a j i", i=RUN),
-                    in_=rows.rearrange("p j (a t i) -> p t a j i", t=PACK, i=RUN)[:, t],
-                )
+        w_codes = {}
+        w_scales = {}
+        for which in ("g", "o"):
+            w_codes[which] = keep.tile([P, PASSES, H], U32, align_bytes=64, name="codes_" + which)
+            w_scales[which] = keep.tile([P, PASSES, H], U8, align_bytes=64, name="scales_" + which)
+        x_codes = keep.tile([P, CHUNKS, PASSES, CHUNK], U32, align_bytes=64)
+        x_scales = keep.tile([P, CHUNKS, PASSES, CHUNK], U8, align_bytes=64)
+        h_codes = keep.tile([P, CHUNKS, PASSES, CHUNK], U32, align_bytes=64)
+        h_scales = keep.tile([P, CHUNKS, PASSES, CHUNK], U8, align_bytes=64)
 
         w_grouped = {}
 
-        def regroup_weight(which, c, half, engine_copy):
-            lay_out = {"g": regroup_permuted, "o": regroup_copy}[which]
-            grouped = stage.tile([P, W_PIECE, PACK], BF16, align_bytes=64, name="w_grouped")
-            lay_out(engine_copy, grouped, w_raw[(which, c, half)][:])
-            w_grouped[(which, c, half)] = grouped
+        def regroup_o(engine_copy, c, cols):
+            if ("o", c) not in w_grouped:
+                w_grouped[("o", c)] = stage.tile([P, H, PACK], BF16, align_bytes=64, name="w_grouped")
+            engine_copy(
+                out=w_grouped[("o", c)][:, cols, :].rearrange("p (a i) j -> p a j i", i=RUN),
+                in_=w_raw[("o", c)][:, :, cols].rearrange("p j (a i) -> p a j i", i=RUN),
+            )
 
-        def quantise_weight(which, c, half):
-            codes, scales = {"g": (wg_codes, wg_scales), "o": (wo_codes, wo_scales)}[which]
-            cols = slice(half * W_PIECE, (half + 1) * W_PIECE)
+        def regroup_g(engine_copy, c, t):
+            if ("g", c) not in w_grouped:
+                w_grouped[("g", c)] = stage.tile([P, H, PACK], BF16, align_bytes=64, name="w_grouped")
+            engine_copy(
+                out=w_grouped[("g", c)][:, t * CHUNK : (t + 1) * CHUNK, :].rearrange("p (a i) j -> p a j i", i=RUN),
+                in_=w_raw[("g", c)][:].rearrange("p j (a t i) -> p t a j i", t=PACK, i=RUN)[:, t],
+            )
+
+        def quantise_weight(which, c, cols=slice(0, H)):
             nc.vector.quantize_mx(
-                out=codes[:, c, cols].bitcast(FP8X4),
-                scales=scales[:, c, cols],
-                in_=w_grouped[(which, c, half)][:].rearrange("p n j -> p (n j)"),
+                out=w_codes[which][:, c, cols].bitcast(FP8X4),
+                scales=w_scales[which][:, c, cols],
+                in_=w_grouped[(which, c)][:, cols, :].rearrange("p n j -> p (n j)"),
             )
 
         x_grouped = {}
 
-        def transpose_x(tt):
+        def transpose_x(tt, engine_copy=nc.scalar.copy):
             ch, tl = divmod(tt, CHUNK_TILES)
             if tl == 0:
-                x_grouped[ch] = stage.tile([P, PASSES * CHUNK * PACK], BF16, align_bytes=64, name="x_grouped")
+                x_grouped[ch] = stage.tile([P, PASSES * CHUNK * PACK], BF16, align_bytes=64, name="x_grouped", bufs=3)
             grouped_words = x_grouped[ch][:].bitcast(F32).rearrange("p (c t u) -> p c t u", c=PASSES, u=2)
-            x_words = x_tiles[tt][:].bitcast(F32)
+            x_words = x_tiles[tt].bitcast(F32)
             xt = psum.tile([P, 2 * PASSES, P], F32, tag="bank")
             for c in range(PASSES):
                 for u in range(2):
                     first = c * 2 * P
                     nc.tensor.transpose(xt[:, 2 * c + u, :], x_words[:, first + u : first + 2 * P : 2], ident_f32[:])
-            nc.scalar.copy(
+            engine_copy(
                 out=grouped_words[:, :, tl * P : (tl + 1) * P, :],
                 in_=xt[:].rearrange("p (c u) t -> p c t u", u=2),
             )
 
         def quantise_x(ch):
-            toks = slice(ch * CHUNK, (ch + 1) * CHUNK)
-            for c in range(PASSES):
-                nc.vector.quantize_mx(
-                    out=x_codes[:, c, toks].bitcast(FP8X4),
-                    scales=x_scales[:, c, toks],
-                    in_=x_grouped[ch][:, c * CHUNK * PACK : (c + 1) * CHUNK * PACK],
-                )
+            nc.vector.quantize_mx(
+                out=x_codes[:, ch].rearrange("p c t -> p (c t)").bitcast(FP8X4),
+                scales=x_scales[:, ch].rearrange("p c t -> p (c t)"),
+                in_=x_grouped[ch][:],
+            )
 
         z_hat = {}
         stats = {}
         moments = {}
+        rstds = {}
+        offsets = {}
 
         def half_stats(tt, a):
             if a == 0:
@@ -201,9 +198,6 @@ def tile_gatedlinearattention_pb_kernel(tc, z, hidden_states, Wg, Wo, gamma, bet
                 moments[ch] = small.tile([P, CHUNK_TILES, 2], F32, name="mean_var")
             nc.vector.bn_aggr(out=moments[ch][:, tl, :], in_=stats[tt][:].rearrange("p a s -> p (a s)"))
 
-        rstds = {}
-        offsets = {}
-
         def invert_deviation(ch):
             var_eps = small.tile([P, CHUNK_TILES], F32)
             nc.gpsimd.tensor_scalar(
@@ -213,23 +207,21 @@ def tile_gatedlinearattention_pb_kernel(tc, z, hidden_states, Wg, Wo, gamma, bet
             nc.gpsimd.tensor_tensor(out=rstd[:], in0=var_eps[:], in1=neg_half[:], op=ALU.pow)
             for tl, tt in enumerate(chunk_tiles(ch)):
                 rstds[tt] = rstd[:, tl : tl + 1]
-                if tt in GPSIMD_TILES:
+                if tt in SCALAR_TILES:
                     offset = small.tile([P, 1], F32)
                     nc.gpsimd.tensor_scalar(
                         out=offset[:], in0=moments[ch][:, tl, 0:1], scalar1=rstds[tt], scalar2=-1.0,
                         op0=ALU.mult, op1=ALU.mult,
                     )
-                    offsets[tt] = offset
+                    offsets[tt] = offset[:]
 
         def normalise(tt):
             ch, tl = divmod(tt, CHUNK_TILES)
             zh = normed.tile([P, H], F32, name="zh")
             permuted = zh[:].rearrange("p (t a i) -> p t a i", t=PACK, i=RUN)
-            z_tile = z_tiles[tt][:].rearrange("p (a t i) -> p t a i", t=PACK, i=RUN)
-            if tt in GPSIMD_TILES:
-                nc.gpsimd.tensor_scalar(
-                    out=permuted, in0=z_tile, scalar1=rstds[tt], scalar2=offsets[tt][:], op0=ALU.mult, op1=ALU.add
-                )
+            z_tile = z_tiles[tt].rearrange("p (a t i) -> p t a i", t=PACK, i=RUN)
+            if tt in SCALAR_TILES:
+                nc.scalar.activation(out=permuted, in_=z_tile, func=ACT.Identity, scale=rstds[tt], bias=offsets[tt])
             else:
                 nc.vector.tensor_scalar(
                     out=permuted, in0=z_tile, scalar1=moments[ch][:, tl, 0:1], scalar2=rstds[tt],
@@ -240,12 +232,13 @@ def tile_gatedlinearattention_pb_kernel(tc, z, hidden_states, Wg, Wo, gamma, bet
         zn_tiles = {}
 
         def transpose_normed(ch):
+            zn = units.tile([P, PACK, PASSES, CHUNK], F32, name="zn")
+            zn_tiles[ch] = zn
             for c2 in range(PASSES):
-                zn = units.tile([P, PACK, CHUNK], F32)
                 for pair in range(PACK // 2):
                     zt = psum.tile([P, 2, CHUNK], F32, tag="bank")
                     for i in range(2):
-                        first = (pair * 2 + i) * PASSES * P + c2 * P
+                        first = (pair * 2 + i) * CHUNK + c2 * P
                         for tl, tt in enumerate(chunk_tiles(ch)):
                             nc.tensor.transpose(
                                 zt[:, i, tl * P : (tl + 1) * P], z_hat[tt][:, first : first + P], ident_f32[:]
@@ -253,155 +246,187 @@ def tile_gatedlinearattention_pb_kernel(tc, z, hidden_states, Wg, Wo, gamma, bet
                     for i in range(2):
                         ft = c2 * PACK + pair * 2 + i
                         nc.scalar.activation(
-                            out=zn[:, pair * 2 + i, :],
+                            out=zn[:, pair * 2 + i, c2, :],
                             in_=zt[:, i, :],
                             func=ACT.Identity,
                             scale=gb_col["gamma"][:, ft : ft + 1],
                             bias=gb_col["beta"][:, ft : ft + 1],
                         )
-                zn_tiles[(ch, c2)] = zn
 
         silu_tiles = {}
 
         def gate_matmul(ch, c2):
-            toks = slice(ch * CHUNK, (ch + 1) * CHUNK)
-            silu_g = units.tile([P, PACK, CHUNK], F32)
+            if ch not in silu_tiles:
+                silu_tiles[ch] = units.tile([P, PACK, PASSES, CHUNK], F32, name="silu")
             for pair in range(PACK // 2):
                 g_bank = psum.tile([P, 2, CHUNK], F32, tag="bank")
                 for i in range(2):
-                    ft = c2 * PACK + pair * 2 + i
+                    first = (pair * 2 + i) * CHUNK + c2 * P
                     for c in range(PASSES):
                         nc.tensor.matmul_mx(
                             out=g_bank[:, i, :],
-                            lhsT=wg_codes[:, c, ft * P : (ft + 1) * P].bitcast(FP8X4),
-                            lhsT_scale=wg_scales[:, c, ft * P : (ft + 1) * P],
-                            rhs=x_codes[:, c, toks].bitcast(FP8X4),
-                            rhs_scale=x_scales[:, c, toks],
+                            lhsT=w_codes["g"][:, c, first : first + P].bitcast(FP8X4),
+                            lhsT_scale=w_scales["g"][:, c, first : first + P],
+                            rhs=x_codes[:, ch, c, :].bitcast(FP8X4),
+                            rhs_scale=x_scales[:, ch, c, :],
                             start=(c == 0),
                             stop=(c == PASSES - 1),
                         )
-                nc.scalar.activation(out=silu_g[:, pair * 2 : pair * 2 + 2, :], in_=g_bank[:], func=ACT.Silu)
-            silu_tiles[(ch, c2)] = silu_g
+                nc.scalar.activation(
+                    out=silu_tiles[ch][:, pair * 2 : pair * 2 + 2, c2, :], in_=g_bank[:], func=ACT.Silu
+                )
 
         h_grouped = {}
 
-        def gate_product(ch, c2, toks=slice(0, CHUNK)):
-            grouped = stage.tile([P, toks.stop - toks.start, PACK], BF16, align_bytes=64, name="h_grouped")
+        def multiply(grouped, zn, silu_g):
             nc.vector.tensor_tensor(
                 out=grouped[:].rearrange("p (a i) j -> p a j i", i=4),
-                in0=zn_tiles[(ch, c2)][:, :, toks].rearrange("p j (a i) -> p a j i", i=4),
-                in1=silu_tiles[(ch, c2)][:, :, toks].rearrange("p j (a i) -> p a j i", i=4),
+                in0=zn.rearrange("p j (a i) -> p a j i", i=4),
+                in1=silu_g.rearrange("p j (a i) -> p a j i", i=4),
                 op=ALU.mult,
             )
+
+        def gate_product(ch, c2=None, toks=slice(0, CHUNK)):
+            if c2 is None:
+                grouped = stage.tile([P, PASSES * CHUNK, PACK], BF16, align_bytes=64, name="h_grouped")
+                multiply(
+                    grouped,
+                    zn_tiles[ch][:].rearrange("p j c t -> p j (c t)"),
+                    silu_tiles[ch][:].rearrange("p j c t -> p j (c t)"),
+                )
+            else:
+                grouped = stage.tile([P, toks.stop - toks.start, PACK], BF16, align_bytes=64, name="h_part", bufs=3)
+                multiply(grouped, zn_tiles[ch][:, :, c2, toks], silu_tiles[ch][:, :, c2, toks])
             h_grouped[(ch, c2, toks.start)] = grouped
 
-        def quantise_h(ch, c2, toks=slice(0, CHUNK)):
-            all_toks = slice(ch * CHUNK + toks.start, ch * CHUNK + toks.stop)
+        def quantise_h(ch, c2=None, toks=slice(0, CHUNK)):
+            if c2 is None:
+                codes = h_codes[:, ch].rearrange("p c t -> p (c t)")
+                scales = h_scales[:, ch].rearrange("p c t -> p (c t)")
+            else:
+                codes, scales = h_codes[:, ch, c2, toks], h_scales[:, ch, c2, toks]
             nc.vector.quantize_mx(
-                out=h_codes[:, c2, all_toks].bitcast(FP8X4),
-                scales=h_scales[:, c2, all_toks],
+                out=codes.bitcast(FP8X4),
+                scales=scales,
                 in_=h_grouped[(ch, c2, toks.start)][:].rearrange("p t j -> p (t j)"),
             )
 
         o_banks = {}
 
-        def project_pass(c2, tiles):
-            for tt in tiles:
-                for first in range(0, H, N_OUT):
-                    if c2 == 0:
-                        o_banks[(tt, first)] = psum.tile([P, N_OUT], F32, tag="bank", name="o_bank")
-                    nc.tensor.matmul_mx(
-                        out=o_banks[(tt, first)][:],
-                        lhsT=h_codes[:, c2, tt * P : (tt + 1) * P].bitcast(FP8X4),
-                        lhsT_scale=h_scales[:, c2, tt * P : (tt + 1) * P],
-                        rhs=wo_codes[:, c2, first : first + N_OUT].bitcast(FP8X4),
-                        rhs_scale=wo_scales[:, c2, first : first + N_OUT],
-                        start=(c2 == 0),
-                        stop=(c2 == PASSES - 1),
-                    )
+        def project_pass(c2, tt):
+            ch, tl = divmod(tt, CHUNK_TILES)
+            toks = slice(tl * P, (tl + 1) * P)
+            for first in range(0, H, N_OUT):
+                if c2 == 0:
+                    o_banks[(tt, first)] = psum.tile([P, N_OUT], F32, tag="bank", name="o_bank")
+                nc.tensor.matmul_mx(
+                    out=o_banks[(tt, first)][:],
+                    lhsT=h_codes[:, ch, c2, toks].bitcast(FP8X4),
+                    lhsT_scale=h_scales[:, ch, c2, toks],
+                    rhs=w_codes["o"][:, c2, first : first + N_OUT].bitcast(FP8X4),
+                    rhs_scale=w_scales["o"][:, c2, first : first + N_OUT],
+                    start=(c2 == 0),
+                    stop=(c2 == PASSES - 1),
+                )
 
-        def drain(tt, first, engine_copy):
-            o_sb = rows.tile([P, N_OUT], F32, tag="row", name="o_sb")
-            engine_copy(out=o_sb[:], in_=o_banks[(tt, first)][:])
-            nc.sync.dma_start(out=out_dram[tt * P : (tt + 1) * P, first : first + N_OUT], in_=o_sb[:])
+        def drain(tt, engines, whole):
+            o_row = rows.tile([P, H], F32, tag="row", name="o_row")
+            for half, engine_copy in enumerate(engines):
+                cols = slice(half * N_OUT, (half + 1) * N_OUT)
+                engine_copy(out=o_row[:, cols], in_=o_banks[(tt, half * N_OUT)][:])
+                if not whole:
+                    nc.sync.dma_start(out=out_dram[:, tt, cols], in_=o_row[:, cols])
+            if whole:
+                nc.sync.dma_start(out=out_dram[:, tt, :], in_=o_row[:])
 
-        for c in range(PASSES):
-            regroup_weight("g", c, 0, nc.vector.tensor_copy)
-            transpose_x(c)
-        for c in range(PASSES):
-            quantise_weight("g", c, 0)
-        regroup_weight("g", 1, 1, nc.vector.tensor_copy)
-        w_grouped[("g", 0, 1)] = stage.tile([P, W_PIECE, PACK], BF16, align_bytes=64, name="w_grouped")
-        for t in range(PACK):
-            regroup_permuted(nc.scalar.copy, w_grouped[("g", 0, 1)], w_raw[("g", 0, 1)][:], (t,))
-            transpose_x(2 + t)
-        quantise_weight("g", 1, 1)
-        quantise_x(0)
+        S, V = nc.scalar.copy, nc.vector.tensor_copy
+        TILE_SLICES = tuple(slice(tl * P, (tl + 1) * P) for tl in range(CHUNK_TILES))
         half_stats(0, 0)
         half_stats(0, 1)
+        transpose_x(0)
+        transpose_x(1)
+        half_stats(1, 0)
+        finish_stats(0)
+        half_stats(1, 1)
+        half_stats(2, 0)
+        finish_stats(1)
+        invert_deviation(0)
+        spread_gamma_beta()
+        half_stats(2, 1)
+        half_stats(3, 0)
+        finish_stats(2)
+        half_stats(3, 1)
+        normalise(0)
+        normalise(1)
+        transpose_x(2)
+        transpose_x(3)
+        transpose_normed(0)
+        half_stats(4, 0)
+        finish_stats(3)
+        invert_deviation(1)
+        half_stats(4, 1)
+        half_stats(5, 0)
+        finish_stats(4)
+        half_stats(5, 1)
+        normalise(2)
+        normalise(3)
+        regroup_g(S, 0, 3)
+        transpose_x(4)
+        transpose_x(5)
+        transpose_normed(1)
+        half_stats(6, 0)
+        finish_stats(5)
+        invert_deviation(2)
+        half_stats(6, 1)
+        half_stats(7, 0)
+        finish_stats(6)
+        half_stats(7, 1)
+        regroup_g(V, 0, 0)
+        finish_stats(7)
+        invert_deviation(3)
+        normalise(4)
+        normalise(5)
+        transpose_normed(2)
+        regroup_g(V, 0, 1)
+        normalise(6)
+        normalise(7)
+        regroup_g(V, 0, 2)
+        quantise_x(0)
         quantise_x(1)
-        quantise_weight("g", 0, 1)
-        gate_matmul(0, 0)
+        quantise_weight("g", 0)
+        regroup_g(V, 1, 0)
+        regroup_g(S, 1, 3)
         transpose_x(6)
         transpose_x(7)
-        gate_matmul(1, 0)
+        regroup_g(V, 1, 1)
+        regroup_g(V, 1, 2)
         quantise_x(2)
-        gate_matmul(2, 0)
-
-        def vector_normalise(ch):
-            for tt in chunk_tiles(ch):
-                if tt not in GPSIMD_TILES:
-                    normalise(tt)
-
-        for tt in range(TOKEN_TILES):
-            if tt > 0:
-                half_stats(tt, 0)
-                finish_stats(tt - 1)
-            if tt in (2, 4, 6):
-                invert_deviation(tt // 2 - 1)
-                for t in chunk_tiles(tt // 2 - 1):
-                    if t in GPSIMD_TILES:
-                        normalise(t)
-            if tt > 0:
-                half_stats(tt, 1)
-            if tt == 1:
-                quantise_x(3)
-                gate_matmul(3, 0)
-                for ch in range(CHUNKS):
-                    gate_matmul(ch, 1)
-                spread_gamma_beta()
-            if tt in (4, 6):
-                vector_normalise(tt // 2 - 2)
-                transpose_normed(tt // 2 - 2)
-        regroup_weight("o", 0, 0, nc.vector.tensor_copy)
-        finish_stats(TOKEN_TILES - 1)
-        invert_deviation(CHUNKS - 1)
-        vector_normalise(2)
-        transpose_normed(2)
-        regroup_weight("o", 0, 1, nc.vector.tensor_copy)
-        regroup_weight("o", 1, 1, nc.scalar.copy)
-        vector_normalise(3)
         transpose_normed(3)
-        for half in range(2):
-            quantise_weight("o", 0, half)
-        regroup_weight("o", 1, 0, nc.vector.tensor_copy)
-        WHOLE = slice(0, CHUNK)
+        quantise_weight("g", 1)
+        quantise_x(3)
+        for ch in range(CHUNKS):
+            gate_matmul(ch, 0)
+            gate_matmul(ch, 1)
+            if ch == 1:
+                regroup_o(S, 1, slice(768, 1024))
+        regroup_o(V, 0, slice(0, 512))
+        regroup_o(V, 0, slice(512, H))
+        quantise_weight("o", 0, slice(0, H))
+        regroup_o(V, 1, slice(0, 768))
+        gate_product(0, 0)
+        quantise_weight("o", 1, slice(0, H))
         steps = []
         for ch in range(CHUNKS):
-            for toks in ((WHOLE,) if ch < 2 else TILE_SLICES):
+            for toks in ((slice(0, CHUNK),) if ch < 1 else TILE_SLICES):
                 for c2 in range(PASSES):
                     steps.append((ch, c2, toks))
-        gate_product(*steps[0])
-        quantise_weight("o", 1, 0)
         for i, (ch, c2, toks) in enumerate(steps):
             if i + 1 < len(steps):
                 gate_product(*steps[i + 1])
-            if i == 1:
-                quantise_weight("o", 1, 1)
             quantise_h(ch, c2, toks)
             tiles = [ch * CHUNK_TILES + t for t in range(toks.start // P, toks.stop // P)]
-            project_pass(c2, tiles)
+            for tt in tiles:
+                project_pass(c2, tt)
             if c2 == PASSES - 1:
                 for tt in tiles:
-                    for first in range(0, H, N_OUT):
-                        drain(tt, first, nc.vector.tensor_copy if (tt, first) in VECTOR_BANKS else nc.scalar.copy)
+                    drain(tt, (S, V if tt == 7 else S), tt < 6)

@@ -93,14 +93,14 @@ def tile_gatedlinearattention_pb_kernel(tc, z, hidden_states, Wg, Wo, gamma, bet
         load_row(z_tiles, z_dram, 1)
         load_chunk(x_tiles, x_dram, 0)
         load_chunk(z_tiles, z_dram, 1)
+        load_chunk(z_tiles, z_dram, 2)
         load_chunk(x_tiles, x_dram, 1)
         load_gamma_beta()
-        load_chunk(z_tiles, z_dram, 2)
         load_chunk(z_tiles, z_dram, 3)
-        load_w("g", Wg, 0)
         load_chunk(x_tiles, x_dram, 2)
-        load_w("g", Wg, 1)
+        load_w("g", Wg, 0)
         load_chunk(x_tiles, x_dram, 3)
+        load_w("g", Wg, 1)
         for c in range(PASSES):
             load_w("o", Wo, c)
 
@@ -128,8 +128,8 @@ def tile_gatedlinearattention_pb_kernel(tc, z, hidden_states, Wg, Wo, gamma, bet
             w_scales[which] = keep.tile([P, PASSES, H], U8, align_bytes=64, name="scales_" + which)
         x_codes = keep.tile([P, CHUNKS, PASSES, CHUNK], U32, align_bytes=64)
         x_scales = keep.tile([P, CHUNKS, PASSES, CHUNK], U8, align_bytes=64)
-        h_codes = keep.tile([P, CHUNKS, PASSES, CHUNK], U32, align_bytes=64)
-        h_scales = keep.tile([P, CHUNKS, PASSES, CHUNK], U8, align_bytes=64)
+        h_codes = keep.tile([P, TOKEN_TILES, PASSES, P], U32, align_bytes=64)
+        h_scales = keep.tile([P, TOKEN_TILES, PASSES, P], U8, align_bytes=64)
 
         w_grouped = {}
 
@@ -232,8 +232,9 @@ def tile_gatedlinearattention_pb_kernel(tc, z, hidden_states, Wg, Wo, gamma, bet
         zn_tiles = {}
 
         def transpose_normed(ch):
-            zn = units.tile([P, PACK, PASSES, CHUNK], F32, name="zn")
-            zn_tiles[ch] = zn
+            zn = units.tile([P, PACK, CHUNK_TILES, PASSES, P], F32, name="zn")
+            for tl, tt in enumerate(chunk_tiles(ch)):
+                zn_tiles[tt] = zn[:, :, tl]
             for c2 in range(PASSES):
                 for pair in range(PACK // 2):
                     zt = psum.tile([P, 2, CHUNK], F32, tag="bank")
@@ -246,18 +247,21 @@ def tile_gatedlinearattention_pb_kernel(tc, z, hidden_states, Wg, Wo, gamma, bet
                     for i in range(2):
                         ft = c2 * PACK + pair * 2 + i
                         nc.scalar.activation(
-                            out=zn[:, pair * 2 + i, c2, :],
-                            in_=zt[:, i, :],
+                            out=zn[:, pair * 2 + i, :, c2, :],
+                            in_=zt[:, i, :].rearrange("p (l t) -> p l t", l=CHUNK_TILES),
                             func=ACT.Identity,
                             scale=gb_col["gamma"][:, ft : ft + 1],
                             bias=gb_col["beta"][:, ft : ft + 1],
                         )
 
         silu_tiles = {}
+        silu_chunks = {}
 
         def gate_matmul(ch, c2):
-            if ch not in silu_tiles:
-                silu_tiles[ch] = units.tile([P, PACK, PASSES, CHUNK], F32, name="silu")
+            if c2 == 0:
+                silu_chunks[ch] = units.tile([P, PACK, CHUNK_TILES, PASSES, P], F32, name="silu")
+                for tl, tt in enumerate(chunk_tiles(ch)):
+                    silu_tiles[tt] = silu_chunks[ch][:, :, tl]
             for pair in range(PACK // 2):
                 g_bank = psum.tile([P, 2, CHUNK], F32, tag="bank")
                 for i in range(2):
@@ -273,7 +277,9 @@ def tile_gatedlinearattention_pb_kernel(tc, z, hidden_states, Wg, Wo, gamma, bet
                             stop=(c == PASSES - 1),
                         )
                 nc.scalar.activation(
-                    out=silu_tiles[ch][:, pair * 2 : pair * 2 + 2, c2, :], in_=g_bank[:], func=ACT.Silu
+                    out=silu_chunks[ch][:, pair * 2 : pair * 2 + 2, :, c2, :],
+                    in_=g_bank[:].rearrange("p j (l t) -> p j l t", l=CHUNK_TILES),
+                    func=ACT.Silu,
                 )
 
         h_grouped = {}
@@ -286,43 +292,36 @@ def tile_gatedlinearattention_pb_kernel(tc, z, hidden_states, Wg, Wo, gamma, bet
                 op=ALU.mult,
             )
 
-        def gate_product(ch, c2=None, toks=slice(0, CHUNK)):
+        def gate_product(tt, c2=None):
             if c2 is None:
-                grouped = stage.tile([P, PASSES * CHUNK, PACK], BF16, align_bytes=64, name="h_grouped")
-                multiply(
-                    grouped,
-                    zn_tiles[ch][:].rearrange("p j c t -> p j (c t)"),
-                    silu_tiles[ch][:].rearrange("p j c t -> p j (c t)"),
-                )
+                grouped = stage.tile([P, PASSES * P, PACK], BF16, align_bytes=64, name="h_grouped", bufs=3)
+                zn, silu_g = [t[tt].rearrange("p j c t -> p j (c t)") for t in (zn_tiles, silu_tiles)]
             else:
-                grouped = stage.tile([P, toks.stop - toks.start, PACK], BF16, align_bytes=64, name="h_part", bufs=3)
-                multiply(grouped, zn_tiles[ch][:, :, c2, toks], silu_tiles[ch][:, :, c2, toks])
-            h_grouped[(ch, c2, toks.start)] = grouped
+                grouped = stage.tile([P, P, PACK], BF16, align_bytes=64, name="h_half")
+                zn, silu_g = [t[tt][:, :, c2, :] for t in (zn_tiles, silu_tiles)]
+            multiply(grouped, zn, silu_g)
+            h_grouped[(tt, c2)] = grouped
 
-        def quantise_h(ch, c2=None, toks=slice(0, CHUNK)):
+        def quantise_h(tt, c2=None):
             if c2 is None:
-                codes = h_codes[:, ch].rearrange("p c t -> p (c t)")
-                scales = h_scales[:, ch].rearrange("p c t -> p (c t)")
+                codes = h_codes[:, tt].rearrange("p c t -> p (c t)")
+                scales = h_scales[:, tt].rearrange("p c t -> p (c t)")
             else:
-                codes, scales = h_codes[:, ch, c2, toks], h_scales[:, ch, c2, toks]
+                codes, scales = h_codes[:, tt, c2, :], h_scales[:, tt, c2, :]
             nc.vector.quantize_mx(
-                out=codes.bitcast(FP8X4),
-                scales=scales,
-                in_=h_grouped[(ch, c2, toks.start)][:].rearrange("p t j -> p (t j)"),
+                out=codes.bitcast(FP8X4), scales=scales, in_=h_grouped[(tt, c2)][:].rearrange("p t j -> p (t j)")
             )
 
         o_banks = {}
 
         def project_pass(c2, tt):
-            ch, tl = divmod(tt, CHUNK_TILES)
-            toks = slice(tl * P, (tl + 1) * P)
             for first in range(0, H, N_OUT):
                 if c2 == 0:
                     o_banks[(tt, first)] = psum.tile([P, N_OUT], F32, tag="bank", name="o_bank")
                 nc.tensor.matmul_mx(
                     out=o_banks[(tt, first)][:],
-                    lhsT=h_codes[:, ch, c2, toks].bitcast(FP8X4),
-                    lhsT_scale=h_scales[:, ch, c2, toks],
+                    lhsT=h_codes[:, tt, c2, :].bitcast(FP8X4),
+                    lhsT_scale=h_scales[:, tt, c2, :],
                     rhs=w_codes["o"][:, c2, first : first + N_OUT].bitcast(FP8X4),
                     rhs_scale=w_scales["o"][:, c2, first : first + N_OUT],
                     start=(c2 == 0),
@@ -340,7 +339,6 @@ def tile_gatedlinearattention_pb_kernel(tc, z, hidden_states, Wg, Wo, gamma, bet
                 nc.sync.dma_start(out=out_dram[:, tt, :], in_=o_row[:])
 
         S, V = nc.scalar.copy, nc.vector.tensor_copy
-        TILE_SLICES = tuple(slice(tl * P, (tl + 1) * P) for tl in range(CHUNK_TILES))
         half_stats(0, 0)
         half_stats(0, 1)
         transpose_x(0)
@@ -351,7 +349,6 @@ def tile_gatedlinearattention_pb_kernel(tc, z, hidden_states, Wg, Wo, gamma, bet
         half_stats(2, 0)
         finish_stats(1)
         invert_deviation(0)
-        spread_gamma_beta()
         half_stats(2, 1)
         half_stats(3, 0)
         finish_stats(2)
@@ -360,6 +357,7 @@ def tile_gatedlinearattention_pb_kernel(tc, z, hidden_states, Wg, Wo, gamma, bet
         normalise(1)
         transpose_x(2)
         transpose_x(3)
+        spread_gamma_beta()
         transpose_normed(0)
         half_stats(4, 0)
         finish_stats(3)
@@ -370,9 +368,9 @@ def tile_gatedlinearattention_pb_kernel(tc, z, hidden_states, Wg, Wo, gamma, bet
         half_stats(5, 1)
         normalise(2)
         normalise(3)
-        regroup_g(S, 0, 3)
         transpose_x(4)
         transpose_x(5)
+        regroup_g(S, 0, 3)
         transpose_normed(1)
         half_stats(6, 0)
         finish_stats(5)
@@ -396,37 +394,66 @@ def tile_gatedlinearattention_pb_kernel(tc, z, hidden_states, Wg, Wo, gamma, bet
         quantise_weight("g", 0)
         regroup_g(V, 1, 0)
         regroup_g(S, 1, 3)
+        regroup_g(S, 1, 2)
         transpose_x(6)
         transpose_x(7)
         regroup_g(V, 1, 1)
-        regroup_g(V, 1, 2)
         quantise_x(2)
         transpose_normed(3)
         quantise_weight("g", 1)
         quantise_x(3)
-        for ch in range(CHUNKS):
-            gate_matmul(ch, 0)
-            gate_matmul(ch, 1)
-            if ch == 1:
-                regroup_o(S, 1, slice(768, 1024))
-        regroup_o(V, 0, slice(0, 512))
-        regroup_o(V, 0, slice(512, H))
-        quantise_weight("o", 0, slice(0, H))
+        regroup_o(S, 1, slice(768, 1024))
+        gate_matmul(0, 0)
+        gate_matmul(0, 1)
+        gate_matmul(1, 0)
+        gate_matmul(1, 1)
+        gate_matmul(2, 0)
+        gate_matmul(2, 1)
+        gate_matmul(3, 0)
+        gate_matmul(3, 1)
+        regroup_o(V, 0, slice(0, H))
+        quantise_weight("o", 0)
         regroup_o(V, 1, slice(0, 768))
-        gate_product(0, 0)
-        quantise_weight("o", 1, slice(0, H))
-        steps = []
-        for ch in range(CHUNKS):
-            for toks in ((slice(0, CHUNK),) if ch < 1 else TILE_SLICES):
-                for c2 in range(PASSES):
-                    steps.append((ch, c2, toks))
-        for i, (ch, c2, toks) in enumerate(steps):
-            if i + 1 < len(steps):
-                gate_product(*steps[i + 1])
-            quantise_h(ch, c2, toks)
-            tiles = [ch * CHUNK_TILES + t for t in range(toks.start // P, toks.stop // P)]
-            for tt in tiles:
-                project_pass(c2, tt)
-            if c2 == PASSES - 1:
-                for tt in tiles:
-                    drain(tt, (S, V if tt == 7 else S), tt < 6)
+        gate_product(0)
+        gate_product(1)
+        quantise_h(0)
+        quantise_weight("o", 1)
+        project_pass(0, 0)
+        project_pass(1, 0)
+        drain(0, (S, S), True)
+        gate_product(2)
+        quantise_h(1)
+        project_pass(0, 1)
+        project_pass(1, 1)
+        drain(1, (S, S), True)
+        gate_product(3)
+        quantise_h(2)
+        project_pass(0, 2)
+        project_pass(1, 2)
+        drain(2, (S, S), True)
+        gate_product(4)
+        quantise_h(3)
+        project_pass(0, 3)
+        project_pass(1, 3)
+        drain(3, (S, S), True)
+        gate_product(5)
+        quantise_h(4)
+        project_pass(0, 4)
+        project_pass(1, 4)
+        drain(4, (S, S), True)
+        gate_product(6)
+        quantise_h(5)
+        project_pass(0, 5)
+        project_pass(1, 5)
+        drain(5, (S, S), True)
+        quantise_h(6)
+        project_pass(0, 6)
+        project_pass(1, 6)
+        gate_product(7, 0)
+        gate_product(7, 1)
+        quantise_h(7, 0)
+        project_pass(0, 7)
+        quantise_h(7, 1)
+        project_pass(1, 7)
+        drain(6, (S, V), False)
+        drain(7, (S, V), False)

@@ -64,9 +64,12 @@ def tile_gatedlinearattention_pb_kernel(tc, z, hidden_states, Wg, Wo, gamma, bet
             for tl, tt in enumerate(chunk_tiles(ch)):
                 tiles[tt] = chunk[:, tl, :]
 
-        def load_row(tiles, dram, tt):
+        def load_row(tiles, dram, tt, width):
             tiles[tt] = rows.tile([P, H], BF16, tag="row", name="row")[:]
-            nc.sync.dma_start(out=tiles[tt], in_=dram[:, tt, :])
+            for first in range(0, H, width):
+                nc.sync.dma_start(
+                    out=tiles[tt][:, first : first + width], in_=dram[:, tt, first : first + width]
+                )
 
         def load_w(which, w_dram, c):
             raw = keep.tile([P, PACK, H], BF16, name="w_raw_%s%d" % (which, c))
@@ -89,8 +92,8 @@ def tile_gatedlinearattention_pb_kernel(tc, z, hidden_states, Wg, Wo, gamma, bet
                         in_=dram[c * K_PASS : (c + 1) * K_PASS].rearrange("(a t i) -> t a i", t=PACK, i=RUN),
                     )
 
-        load_row(z_tiles, z_dram, 0)
-        load_row(z_tiles, z_dram, 1)
+        load_row(z_tiles, z_dram, 0, BN_WIDTH)
+        load_row(z_tiles, z_dram, 1, H)
         load_chunk(x_tiles, x_dram, 0)
         load_chunk(z_tiles, z_dram, 1)
         load_chunk(z_tiles, z_dram, 2)
@@ -141,12 +144,12 @@ def tile_gatedlinearattention_pb_kernel(tc, z, hidden_states, Wg, Wo, gamma, bet
                 in_=w_raw[("o", c)][:, :, cols].rearrange("p j (a i) -> p a j i", i=RUN),
             )
 
-        def regroup_g(engine_copy, c, t):
+        def regroup_g(engine_copy, c, parts):
             if ("g", c) not in w_grouped:
                 w_grouped[("g", c)] = stage.tile([P, H, PACK], BF16, align_bytes=64, name="w_grouped")
             engine_copy(
-                out=w_grouped[("g", c)][:, t * CHUNK : (t + 1) * CHUNK, :].rearrange("p (a i) j -> p a j i", i=RUN),
-                in_=w_raw[("g", c)][:].rearrange("p j (a t i) -> p t a j i", t=PACK, i=RUN)[:, t],
+                out=w_grouped[("g", c)][:].rearrange("p (t a i) j -> p t a j i", t=PACK, i=RUN)[:, parts],
+                in_=w_raw[("g", c)][:].rearrange("p j (a t i) -> p t a j i", t=PACK, i=RUN)[:, parts],
             )
 
         def quantise_weight(which, c, cols=slice(0, H)):
@@ -231,24 +234,25 @@ def tile_gatedlinearattention_pb_kernel(tc, z, hidden_states, Wg, Wo, gamma, bet
 
         zn_tiles = {}
 
-        def transpose_normed(ch):
-            zn = units.tile([P, PACK, CHUNK_TILES, PASSES, P], F32, name="zn")
-            for tl, tt in enumerate(chunk_tiles(ch)):
-                zn_tiles[tt] = zn[:, :, tl]
+        def transpose_normed(first_tile, tiles):
+            zn = units.tile([P, PACK, tiles, PASSES, P], F32, name="zn%d" % first_tile, bufs=1)
+            for tl in range(tiles):
+                zn_tiles[first_tile + tl] = zn[:, :, tl]
+            per_bank = N_OUT // (tiles * P)
             for c2 in range(PASSES):
-                for pair in range(PACK // 2):
-                    zt = psum.tile([P, 2, CHUNK], F32, tag="bank")
-                    for i in range(2):
-                        first = (pair * 2 + i) * CHUNK + c2 * P
-                        for tl, tt in enumerate(chunk_tiles(ch)):
+                for j0 in range(0, PACK, per_bank):
+                    zt = psum.tile([P, per_bank, tiles, P], F32, tag="bank")
+                    for i in range(per_bank):
+                        first = (j0 + i) * CHUNK + c2 * P
+                        for tl in range(tiles):
                             nc.tensor.transpose(
-                                zt[:, i, tl * P : (tl + 1) * P], z_hat[tt][:, first : first + P], ident_f32[:]
+                                zt[:, i, tl, :], z_hat[first_tile + tl][:, first : first + P], ident_f32[:]
                             )
-                    for i in range(2):
-                        ft = c2 * PACK + pair * 2 + i
+                    for i in range(per_bank):
+                        ft = c2 * PACK + j0 + i
                         nc.scalar.activation(
-                            out=zn[:, pair * 2 + i, :, c2, :],
-                            in_=zt[:, i, :].rearrange("p (l t) -> p l t", l=CHUNK_TILES),
+                            out=zn[:, j0 + i, :, c2, :],
+                            in_=zt[:, i],
                             func=ACT.Identity,
                             scale=gb_col["gamma"][:, ft : ft + 1],
                             bias=gb_col["beta"][:, ft : ft + 1],
@@ -328,6 +332,10 @@ def tile_gatedlinearattention_pb_kernel(tc, z, hidden_states, Wg, Wo, gamma, bet
                     stop=(c2 == PASSES - 1),
                 )
 
+        def project(tt):
+            for c2 in range(PASSES):
+                project_pass(c2, tt)
+
         def drain(tt, engines, whole):
             o_row = rows.tile([P, H], F32, tag="row", name="o_row")
             for half, engine_copy in enumerate(engines):
@@ -358,7 +366,7 @@ def tile_gatedlinearattention_pb_kernel(tc, z, hidden_states, Wg, Wo, gamma, bet
         transpose_x(2)
         transpose_x(3)
         spread_gamma_beta()
-        transpose_normed(0)
+        transpose_normed(0, 2)
         half_stats(4, 0)
         finish_stats(3)
         invert_deviation(1)
@@ -370,8 +378,8 @@ def tile_gatedlinearattention_pb_kernel(tc, z, hidden_states, Wg, Wo, gamma, bet
         normalise(3)
         transpose_x(4)
         transpose_x(5)
-        regroup_g(S, 0, 3)
-        transpose_normed(1)
+        regroup_g(S, 0, slice(3, 4))
+        transpose_normed(2, 2)
         half_stats(6, 0)
         finish_stats(5)
         invert_deviation(2)
@@ -379,27 +387,23 @@ def tile_gatedlinearattention_pb_kernel(tc, z, hidden_states, Wg, Wo, gamma, bet
         half_stats(7, 0)
         finish_stats(6)
         half_stats(7, 1)
-        regroup_g(V, 0, 0)
+        regroup_g(V, 0, slice(2, 3))
         finish_stats(7)
         invert_deviation(3)
         normalise(4)
         normalise(5)
-        transpose_normed(2)
-        regroup_g(V, 0, 1)
+        regroup_g(V, 0, slice(0, 2))
         normalise(6)
         normalise(7)
-        regroup_g(V, 0, 2)
         quantise_x(0)
         quantise_x(1)
         quantise_weight("g", 0)
-        regroup_g(V, 1, 0)
-        regroup_g(S, 1, 3)
-        regroup_g(S, 1, 2)
+        regroup_g(V, 1, slice(0, 2))
+        regroup_g(S, 1, slice(2, 4))
         transpose_x(6)
         transpose_x(7)
-        regroup_g(V, 1, 1)
         quantise_x(2)
-        transpose_normed(3)
+        transpose_normed(4, 4)
         quantise_weight("g", 1)
         quantise_x(3)
         regroup_o(S, 1, slice(768, 1024))

from contextlib import ExitStack

import concourse.mybir as mybir
from concourse.masks import make_identity

F32 = mybir.dt.float32
BF16 = mybir.dt.bfloat16
U32 = mybir.dt.uint32
U8 = mybir.dt.uint8
FP8X4 = mybir.dt.float8_e4m3fn_x4
ALU = mybir.AluOpType
ACT = mybir.ActivationFunctionType

P = 128
PACK = 4
RUN = 4
K_PASS = P * PACK
TOKENS = 1024
H = 1024
PASSES = H // K_PASS
TOKEN_TILES = TOKENS // P
FEATURE_TILES = H // P
CHUNK_TILES = 2
CHUNK = CHUNK_TILES * P
CHUNKS = TOKENS // CHUNK
N_OUT = 512
LN_EPS = 1e-5
SCALAR_TILES = (1,)
BN_WIDTH = 512

FLOPS = 2 * 2 * TOKENS * H * H


def tile_gatedlinearattention_pb_kernel(tc, z, hidden_states, Wg, Wo, gamma, beta, out):
    nc = tc.nc
    x_dram = hidden_states.flatten_outer_dims().rearrange("(p t) k -> p t k", t=TOKEN_TILES)
    z_dram = z.flatten_outer_dims().rearrange("(p t) k -> p t k", t=TOKEN_TILES)
    out_dram = out.flatten_outer_dims().rearrange("(p t) m -> p t m", t=TOKEN_TILES)

    with ExitStack() as ctx:
        ctx.enter_context(tc.manual_schedule())
        keep = ctx.enter_context(tc.tile_pool(name="keep", bufs=1))
        stage = ctx.enter_context(tc.tile_pool(name="stage", bufs=2))
        small = ctx.enter_context(tc.tile_pool(name="small", bufs=TOKEN_TILES))
        normed = ctx.enter_context(tc.tile_pool(name="normed", bufs=6))
        units = ctx.enter_context(tc.tile_pool(name="units", bufs=CHUNKS))
        rows = ctx.enter_context(tc.tile_pool(name="rows", bufs=2 * CHUNKS + 1))
        psum = ctx.enter_context(tc.psum_pool(name="psum", bufs=8))

        def chunk_tiles(ch):
            return range(ch * CHUNK_TILES, (ch + 1) * CHUNK_TILES)

        z_tiles = {}
        x_tiles = {}
        w_raw = {}
        gb_rows = {}
        for which in ("gamma", "beta"):
            gb_rows[which] = keep.tile([P, P], BF16, name="rows_" + which)
            nc.gpsimd.memset(gb_rows[which][:], 0.0)

        def load_chunk(tiles, dram, ch):
            chunk = rows.tile([P, CHUNK_TILES, H], BF16, tag="row", name="row")
            nc.sync.dma_start(out=chunk[:], in_=dram[:, ch * CHUNK_TILES : (ch + 1) * CHUNK_TILES, :])
            for tl, tt in enumerate(chunk_tiles(ch)):
                tiles[tt] = chunk[:, tl, :]

        def load_row(tiles, dram, tt, width):
            tiles[tt] = rows.tile([P, H], BF16, tag="row", name="row")[:]
            for first in range(0, H, width):
                nc.sync.dma_start(
                    out=tiles[tt][:, first : first + width], in_=dram[:, tt, first : first + width]
                )

        def load_w(which, w_dram, c):
            raw = keep.tile([P, PACK, H], BF16, name="w_raw_%s%d" % (which, c))
            piece = w_dram[c * K_PASS : (c + 1) * K_PASS, :]
            if which == "g":
                nc.sync.dma_start(out=raw[:], in_=piece.rearrange("(p j) n -> p j n", j=PACK))
            else:
                for i in range(RUN):
                    nc.sync.dma_start(
                        out=raw[i:P:RUN],
                        in_=piece.rearrange("(a j i) n -> i a j n", j=PACK, i=RUN)[i],
                    )
            w_raw[(which, c)] = raw

        def load_gamma_beta():
            for which, dram in (("gamma", gamma), ("beta", beta)):
                for c in range(PASSES):
                    nc.sync.dma_start(
                        out=gb_rows[which][c * PACK : (c + 1) * PACK, :].rearrange("t (a i) -> t a i", i=RUN),
                        in_=dram[c * K_PASS : (c + 1) * K_PASS].rearrange("(a t i) -> t a i", t=PACK, i=RUN),
                    )

        load_row(z_tiles, z_dram, 0, BN_WIDTH)
        load_row(z_tiles, z_dram, 1, H)
        load_chunk(x_tiles, x_dram, 0)
        load_chunk(z_tiles, z_dram, 1)
        load_chunk(z_tiles, z_dram, 2)
        load_chunk(x_tiles, x_dram, 1)
        load_gamma_beta()
        load_chunk(z_tiles, z_dram, 3)
        load_chunk(x_tiles, x_dram, 2)
        load_w("g", Wg, 0)
        load_chunk(x_tiles, x_dram, 3)
        load_w("g", Wg, 1)
        for c in range(PASSES):
            load_w("o", Wo, c)

        neg_half = keep.tile([P, CHUNK_TILES], F32)
        nc.gpsimd.memset(neg_half[:], -0.5)
        warm = keep.tile([P, 1], F32)
        nc.scalar.activation(out=warm[:], in_=neg_half[:, 0:1], func=ACT.Silu)
        ident_f32 = keep.tile([P, P], F32)
        make_identity(nc, ident_f32[:])
        ident_bf16 = keep.tile([P, P], BF16)
        make_identity(nc, ident_bf16[:])
        gb_col = {}

        def spread_gamma_beta():
            for which in ("gamma", "beta"):
                gb_t = psum.tile([P, P], BF16, tag="bank")
                nc.tensor.transpose(gb_t[:], gb_rows[which][:], ident_bf16[:])
                gb_col[which] = keep.tile([P, FEATURE_TILES], F32, name="col_" + which)
                nc.scalar.copy(out=gb_col[which][:], in_=gb_t[:, 0:FEATURE_TILES])

        w_codes = {}
        w_scales = {}
        for which in ("g", "o"):
            w_codes[which] = keep.tile([P, PASSES, H], U32, align_bytes=64, name="codes_" + which)
            w_scales[which] = keep.tile([P, PASSES, H], U8, align_bytes=64, name="scales_" + which)
        x_codes = keep.tile([P, CHUNKS, PASSES, CHUNK], U32, align_bytes=64)
        x_scales = keep.tile([P, CHUNKS, PASSES, CHUNK], U8, align_bytes=64)
        h_codes = keep.tile([P, TOKEN_TILES, PASSES, P], U32, align_bytes=64)
        h_scales = keep.tile([P, TOKEN_TILES, PASSES, P], U8, align_bytes=64)

        w_grouped = {}

        def regroup_o(engine_copy, c, cols):
            if ("o", c) not in w_grouped:
                w_grouped[("o", c)] = stage.tile([P, H, PACK], BF16, align_bytes=64, name="w_grouped")
            engine_copy(
                out=w_grouped[("o", c)][:, cols, :].rearrange("p (a i) j -> p a j i", i=RUN),
                in_=w_raw[("o", c)][:, :, cols].rearrange("p j (a i) -> p a j i", i=RUN),
            )

        def regroup_g(engine_copy, c, parts):
            if ("g", c) not in w_grouped:
                w_grouped[("g", c)] = stage.tile([P, H, PACK], BF16, align_bytes=64, name="w_grouped")
            engine_copy(
                out=w_grouped[("g", c)][:].rearrange("p (t a i) j -> p t a j i", t=PACK, i=RUN)[:, parts],
                in_=w_raw[("g", c)][:].rearrange("p j (a t i) -> p t a j i", t=PACK, i=RUN)[:, parts],
            )

        def quantise_weight(which, c, cols=slice(0, H)):
            nc.vector.quantize_mx(
                out=w_codes[which][:, c, cols].bitcast(FP8X4),
                scales=w_scales[which][:, c, cols],
                in_=w_grouped[(which, c)][:, cols, :].rearrange("p n j -> p (n j)"),
            )

        x_grouped = {}

        def transpose_x(tt, engine_copy=nc.scalar.copy):
            ch, tl = divmod(tt, CHUNK_TILES)
            if tl == 0:
                x_grouped[ch] = stage.tile([P, PASSES * CHUNK * PACK], BF16, align_bytes=64, name="x_grouped", bufs=3)
            grouped_words = x_grouped[ch][:].bitcast(F32).rearrange("p (c t u) -> p c t u", c=PASSES, u=2)
            x_words = x_tiles[tt].bitcast(F32)
            xt = psum.tile([P, 2 * PASSES, P], F32, tag="bank")
            for c in range(PASSES):
                for u in range(2):
                    first = c * 2 * P
                    nc.tensor.transpose(xt[:, 2 * c + u, :], x_words[:, first + u : first + 2 * P : 2], ident_f32[:])
            engine_copy(
                out=grouped_words[:, :, tl * P : (tl + 1) * P, :],
                in_=xt[:].rearrange("p (c u) t -> p c t u", u=2),
            )

        def quantise_x(ch):
            nc.vector.quantize_mx(
                out=x_codes[:, ch].rearrange("p c t -> p (c t)").bitcast(FP8X4),
                scales=x_scales[:, ch].rearrange("p c t -> p (c t)"),
                in_=x_grouped[ch][:],
            )

        z_hat = {}
        stats = {}
        moments = {}
        rstds = {}
        offsets = {}

        def half_stats(tt, a):
            if a == 0:
                stats[tt] = small.tile([P, H // BN_WIDTH, 6], F32, name="stats")
            nc.vector.bn_stats(out=stats[tt][:, a, :], in_=z_tiles[tt][:, a * BN_WIDTH : (a + 1) * BN_WIDTH])

        def finish_stats(tt):
            ch, tl = divmod(tt, CHUNK_TILES)
            if tl == 0:
                moments[ch] = small.tile([P, CHUNK_TILES, 2], F32, name="mean_var")
            nc.vector.bn_aggr(out=moments[ch][:, tl, :], in_=stats[tt][:].rearrange("p a s -> p (a s)"))

        def invert_deviation(ch):
            var_eps = small.tile([P, CHUNK_TILES], F32)
            nc.gpsimd.tensor_scalar(
                out=var_eps[:], in0=moments[ch][:, :, 1], scalar1=1.0, scalar2=LN_EPS, op0=ALU.mult, op1=ALU.add
            )
            rstd = small.tile([P, CHUNK_TILES], F32)
            nc.gpsimd.tensor_tensor(out=rstd[:], in0=var_eps[:], in1=neg_half[:], op=ALU.pow)
            for tl, tt in enumerate(chunk_tiles(ch)):
                rstds[tt] = rstd[:, tl : tl + 1]
                if tt in SCALAR_TILES:
                    offset = small.tile([P, 1], F32)
                    nc.gpsimd.tensor_scalar(
                        out=offset[:], in0=moments[ch][:, tl, 0:1], scalar1=rstds[tt], scalar2=-1.0,
                        op0=ALU.mult, op1=ALU.mult,
                    )
                    offsets[tt] = offset[:]

        def normalise(tt):
            ch, tl = divmod(tt, CHUNK_TILES)
            zh = normed.tile([P, H], F32, name="zh")
            permuted = zh[:].rearrange("p (t a i) -> p t a i", t=PACK, i=RUN)
            z_tile = z_tiles[tt].rearrange("p (a t i) -> p t a i", t=PACK, i=RUN)
            if tt in SCALAR_TILES:
                nc.scalar.activation(out=permuted, in_=z_tile, func=ACT.Identity, scale=rstds[tt], bias=offsets[tt])
            else:
                nc.vector.tensor_scalar(
                    out=permuted, in0=z_tile, scalar1=moments[ch][:, tl, 0:1], scalar2=rstds[tt],
                    op0=ALU.subtract, op1=ALU.mult,
                )
            z_hat[tt] = zh

        zn_tiles = {}

        def transpose_normed(first_tile, tiles):
            zn = units.tile([P, PACK, tiles, PASSES, P], F32, name="zn%d" % first_tile, bufs=1)
            for tl in range(tiles):
                zn_tiles[first_tile + tl] = zn[:, :, tl]
            per_bank = N_OUT // (tiles * P)
            for c2 in range(PASSES):
                for j0 in range(0, PACK, per_bank):
                    zt = psum.tile([P, per_bank, tiles, P], F32, tag="bank")
                    for i in range(per_bank):
                        first = (j0 + i) * CHUNK + c2 * P
                        for tl in range(tiles):
                            nc.tensor.transpose(
                                zt[:, i, tl, :], z_hat[first_tile + tl][:, first : first + P], ident_f32[:]
                            )
                    for i in range(per_bank):
                        ft = c2 * PACK + j0 + i
                        nc.scalar.activation(
                            out=zn[:, j0 + i, :, c2, :],
                            in_=zt[:, i],
                            func=ACT.Identity,
                            scale=gb_col["gamma"][:, ft : ft + 1],
                            bias=gb_col["beta"][:, ft : ft + 1],
                        )

        silu_tiles = {}
        silu_chunks = {}

        def gate_matmul(ch, c2):
            if c2 == 0:
                silu_chunks[ch] = units.tile([P, PACK, CHUNK_TILES, PASSES, P], F32, name="silu")
                for tl, tt in enumerate(chunk_tiles(ch)):
                    silu_tiles[tt] = silu_chunks[ch][:, :, tl]
            for pair in range(PACK // 2):
                g_bank = psum.tile([P, 2, CHUNK], F32, tag="bank")
                for i in range(2):
                    first = (pair * 2 + i) * CHUNK + c2 * P
                    for c in range(PASSES):
                        nc.tensor.matmul_mx(
                            out=g_bank[:, i, :],
                            lhsT=w_codes["g"][:, c, first : first + P].bitcast(FP8X4),
                            lhsT_scale=w_scales["g"][:, c, first : first + P],
                            rhs=x_codes[:, ch, c, :].bitcast(FP8X4),
                            rhs_scale=x_scales[:, ch, c, :],
                            start=(c == 0),
                            stop=(c == PASSES - 1),
                        )
                nc.scalar.activation(
                    out=silu_chunks[ch][:, pair * 2 : pair * 2 + 2, :, c2, :],
                    in_=g_bank[:].rearrange("p j (l t) -> p j l t", l=CHUNK_TILES),
                    func=ACT.Silu,
                )

        h_grouped = {}

        def multiply(grouped, zn, silu_g):
            nc.vector.tensor_tensor(
                out=grouped[:].rearrange("p (a i) j -> p a j i", i=4),
                in0=zn.rearrange("p j (a i) -> p a j i", i=4),
                in1=silu_g.rearrange("p j (a i) -> p a j i", i=4),
                op=ALU.mult,
            )

        def gate_product(tt, c2=None):
            if c2 is None:
                grouped = stage.tile([P, PASSES * P, PACK], BF16, align_bytes=64, name="h_grouped", bufs=3)
                zn, silu_g = [t[tt].rearrange("p j c t -> p j (c t)") for t in (zn_tiles, silu_tiles)]
            else:
                grouped = stage.tile([P, P, PACK], BF16, align_bytes=64, name="h_half")
                zn, silu_g = [t[tt][:, :, c2, :] for t in (zn_tiles, silu_tiles)]
            multiply(grouped, zn, silu_g)
            h_grouped[(tt, c2)] = grouped

        def quantise_h(tt, c2=None):
            if c2 is None:
                codes = h_codes[:, tt].rearrange("p c t -> p (c t)")
                scales = h_scales[:, tt].rearrange("p c t -> p (c t)")
            else:
                codes, scales = h_codes[:, tt, c2, :], h_scales[:, tt, c2, :]
            nc.vector.quantize_mx(
                out=codes.bitcast(FP8X4), scales=scales, in_=h_grouped[(tt, c2)][:].rearrange("p t j -> p (t j)")
            )

        o_banks = {}

        def project_pass(c2, tt):
            for first in range(0, H, N_OUT):
                if c2 == 0:
                    o_banks[(tt, first)] = psum.tile([P, N_OUT], F32, tag="bank", name="o_bank")
                nc.tensor.matmul_mx(
                    out=o_banks[(tt, first)][:],
                    lhsT=h_codes[:, tt, c2, :].bitcast(FP8X4),
                    lhsT_scale=h_scales[:, tt, c2, :],
                    rhs=w_codes["o"][:, c2, first : first + N_OUT].bitcast(FP8X4),
                    rhs_scale=w_scales["o"][:, c2, first : first + N_OUT],
                    start=(c2 == 0),
                    stop=(c2 == PASSES - 1),
                )

        def project(tt):
            for c2 in range(PASSES):
                project_pass(c2, tt)

        def drain(tt, engines, whole):
            o_row = rows.tile([P, H], F32, tag="row", name="o_row")
            for half, engine_copy in enumerate(engines):
                cols = slice(half * N_OUT, (half + 1) * N_OUT)
                engine_copy(out=o_row[:, cols], in_=o_banks[(tt, half * N_OUT)][:])
                if not whole:
                    nc.sync.dma_start(out=out_dram[:, tt, cols], in_=o_row[:, cols])
            if whole:
                nc.sync.dma_start(out=out_dram[:, tt, :], in_=o_row[:])

        S, V = nc.scalar.copy, nc.vector.tensor_copy
        half_stats(0, 0)
        half_stats(0, 1)
        transpose_x(0)
        transpose_x(1)
        half_stats(1, 0)
        finish_stats(0)
        half_stats(1, 1)
        half_stats(2, 0)
        finish_stats(1)
        invert_deviation(0)
        half_stats(2, 1)
        half_stats(3, 0)
        finish_stats(2)
        half_stats(3, 1)
        normalise(0)
        normalise(1)
        transpose_x(2)
        transpose_x(3)
        spread_gamma_beta()
        transpose_normed(0, 2)
        half_stats(4, 0)
        finish_stats(3)
        invert_deviation(1)
        half_stats(4, 1)
        half_stats(5, 0)
        finish_stats(4)
        half_stats(5, 1)
        normalise(2)
        normalise(3)
        transpose_x(4)
        transpose_x(5)
        regroup_g(S, 0, slice(3, 4))
        transpose_normed(2, 2)
        half_stats(6, 0)
        finish_stats(5)
        invert_deviation(2)
        half_stats(6, 1)
        half_stats(7, 0)
        finish_stats(6)
        half_stats(7, 1)
        regroup_g(V, 0, slice(2, 3))
        finish_stats(7)
        invert_deviation(3)
        normalise(4)
        normalise(5)
        regroup_g(V, 0, slice(0, 2))
        normalise(6)
        normalise(7)
        quantise_x(0)
        quantise_x(1)
        quantise_weight("g", 0)
        regroup_g(V, 1, slice(0, 2))
        regroup_g(S, 1, slice(2, 4))
        transpose_x(6)
        transpose_x(7)
        quantise_x(2)
        transpose_normed(4, 4)
        quantise_weight("g", 1)
        quantise_x(3)
        regroup_o(S, 1, slice(768, 1024))
        gate_matmul(0, 0)
        gate_matmul(0, 1)
        gate_matmul(1, 0)
        gate_matmul(1, 1)
        gate_matmul(2, 0)
        gate_matmul(2, 1)
        gate_matmul(3, 0)
        gate_matmul(3, 1)
        regroup_o(V, 0, slice(0, H))
        quantise_weight("o", 0)
        regroup_o(V, 1, slice(0, 768))
        gate_product(0)
        gate_product(1)
        quantise_h(0)
        quantise_weight("o", 1)
        project_pass(0, 0)
        project_pass(1, 0)
        drain(0, (S, S), True)
        gate_product(2)
        quantise_h(1)
        project_pass(0, 1)
        project_pass(1, 1)
        drain(1, (S, S), True)
        gate_product(3)
        quantise_h(2)
        project_pass(0, 2)
        project_pass(1, 2)
        drain(2, (S, S), True)
        gate_product(4)
        quantise_h(3)
        project_pass(0, 3)
        project_pass(1, 3)
        drain(3, (S, S), True)
        gate_product(5)
        quantise_h(4)
        project_pass(0, 4)
        project_pass(1, 4)
        drain(4, (S, S), True)
        gate_product(6)
        quantise_h(5)
        project_pass(0, 5)
        project_pass(1, 5)
        drain(5, (S, S), True)
        quantise_h(6)
        project_pass(0, 6)
        project_pass(1, 6)
        gate_product(7, 0)
        gate_product(7, 1)
        quantise_h(7, 0)
        project_pass(0, 7)
        quantise_h(7, 1)
        project_pass(1, 7)
        drain(6, (S, V), False)
        drain(7, (S, V), False)
